import numpy as np
import ml_dtypes


def mxq(x, axis, fmt="e4m3"):
    dtype, down = {"e4m3": (ml_dtypes.float8_e4m3fn, 7), "e5m2": (ml_dtypes.float8_e5m2, 14)}[fmt]
    v = np.moveaxis(np.asarray(x, np.float32).astype(ml_dtypes.bfloat16).astype(np.float64), axis, -1)
    blocks = v.reshape(v.shape[:-1] + (-1, 32))
    amax = np.abs(blocks).max(-1, keepdims=True)
    byte = np.maximum(np.where(amax > 0, np.frexp(amax)[1] - 1 + 127, 0) - down, 1)
    scale = np.exp2(byte - 127.0)
    codes = (blocks / scale).astype(np.float32).astype(dtype).astype(np.float64)
    return np.moveaxis((codes * scale).reshape(v.shape), -1, axis)


WIDE = False


def mx_kscale(k):
    if not WIDE:
        return np.ones(k)
    levels = np.array([10, -10, 5, -5, 0])
    a = np.random.permutation(np.resize(levels, k // 512 * 4)).reshape(k // 512, 4)
    idx = np.arange(k)
    return np.exp2(a[idx // 512, idx % 128 // 32])


BF16 = ml_dtypes.bfloat16


def bf(x):
    return np.asarray(x, np.float32).astype(BF16)


def f64(x):
    return np.asarray(x).astype(np.float64)


B, S, D, H, KVH, HD = 1, 512, 2048, 16, 4, 128
E = H * HD
KV = KVH * HD
EPS = 1e-6


def layernorm(u, gamma, beta):
    mu = u.mean(-1, keepdims=True)
    var = np.square(u - mu).mean(-1, keepdims=True)
    return (u - mu) / np.sqrt(var + EPS) * gamma + beta


def apply_rope(u, cos, sin):
    half = u.shape[-1] // 2
    rotated = np.concatenate([-u[..., half:], u[..., :half]], axis=-1)
    return u * cos[None, None] + rotated * sin[None, None]


def setup_inputs():
    s = mx_kscale(D)
    return {
        "x": bf(np.random.standard_normal((B, S, D)) * s),
        "cos": bf(np.random.uniform(size=(S, HD))),
        "sin": bf(np.random.uniform(size=(S, HD))),
        "Wq": bf(np.random.standard_normal((D, E)) / np.sqrt(D) / s[:, None]),
        "Wk": bf(np.random.standard_normal((D, KV)) / np.sqrt(D) / s[:, None]),
        "Wv": bf(np.random.standard_normal((D, KV)) * 2.0 / np.sqrt(D) / s[:, None]),
        "q_gamma": bf(1.0 + 0.1 * np.random.standard_normal(HD)),
        "q_beta": bf(0.1 * np.random.standard_normal(HD)),
        "k_gamma": bf(1.0 + 0.1 * np.random.standard_normal(HD)),
        "k_beta": bf(0.1 * np.random.standard_normal(HD)),
    }


def reference(x, cos, sin, Wq, Wk, Wv, q_gamma, q_beta, k_gamma, k_beta):
    xq = mxq(f64(x), 2, "e4m3")
    q = (xq @ mxq(f64(Wq), 0, "e4m3")).reshape(B, S, H, HD).transpose(0, 2, 1, 3)
    k = (xq @ mxq(f64(Wk), 0, "e4m3")).reshape(B, S, KVH, HD).transpose(0, 2, 1, 3)
    v = (xq @ mxq(f64(Wv), 0, "e4m3")).reshape(B, S, KVH, HD).transpose(0, 2, 1, 3)
    q = layernorm(q, f64(q_gamma), f64(q_beta))
    k = layernorm(k, f64(k_gamma), f64(k_beta))
    q_rot = apply_rope(q, f64(cos), f64(sin))
    k_rot = apply_rope(k, f64(cos), f64(sin))
    return q_rot, k_rot, v

@@ -1,0 +1,309 @@
+from contextlib import ExitStack
+
+import concourse.mybir as mybir
+from concourse.masks import make_identity
+
+F32 = mybir.dt.float32
+BF16 = mybir.dt.bfloat16
+U32 = mybir.dt.uint32
+U8 = mybir.dt.uint8
+FP8X4 = mybir.dt.float8_e4m3fn_x4
+ALU = mybir.AluOpType
+ACT = mybir.ActivationFunctionType
+
+P = 128
+PACK = 4
+K_PASS = P * PACK
+TOKENS = 512
+TOKEN_TILES = TOKENS // P
+D_MODEL = 2048
+PASSES = D_MODEL // K_PASS
+HEAD = 128
+HALF = HEAD // 2
+BLOCK_HEADS = 4
+BLOCK = BLOCK_HEADS * HEAD
+UNITS = BLOCK_HEADS * TOKEN_TILES
+Q_BLOCKS = 4
+EPS = 1e-6
+LOAD_AHEAD = 3
+VECTOR_COPIES_AT_START = 2
+VECTOR_COPIES_LATER = 1
+
+FLOPS = 2 * TOKENS * D_MODEL * (Q_BLOCKS + 2) * BLOCK
+
+
+def add_partner_halves(nc, out, products):
+    for lo, partner in ((0, HALF), (HALF, 0)):
+        nc.vector.tensor_tensor(
+            out=out[:, :, lo : lo + HALF],
+            in0=products[:, :, 0, lo : lo + HALF],
+            in1=products[:, :, 1, partner : partner + HALF],
+            op=ALU.add,
+        )
+
+
+def tile_gqa_flashattn_pa_kernel(
+    tc, x, cos, sin, Wq, Wk, Wv, q_gamma, q_beta, k_gamma, k_beta, q_rot, k_rot, v_out
+):
+    nc = tc.nc
+    with ExitStack() as ctx:
+        ctx.enter_context(tc.manual_schedule())
+        const = ctx.enter_context(tc.tile_pool(name="const", bufs=1))
+        raw_pool = ctx.enter_context(tc.tile_pool(name="raw", bufs=LOAD_AHEAD * PASSES))
+        grouped_pool = ctx.enter_context(tc.tile_pool(name="grouped", bufs=2 * PASSES))
+        codes_pool = ctx.enter_context(tc.tile_pool(name="codes", bufs=2))
+        stats_pool = ctx.enter_context(tc.tile_pool(name="stats", bufs=3))
+        result_pool = ctx.enter_context(tc.tile_pool(name="result", bufs=2))
+        psum = ctx.enter_context(tc.psum_pool(name="psum", bufs=8))
+
+        def heads_of(out):
+            return out.rearrange("o h (p i) j -> p (o h) (i j)", i=TOKEN_TILES)
+
+        blocks = [(Wk, heads_of(k_rot), "k")]
+        for c in range(Q_BLOCKS):
+            blocks.append(
+                (
+                    Wq[:, c * BLOCK : (c + 1) * BLOCK],
+                    heads_of(q_rot)[:, c * BLOCK_HEADS : (c + 1) * BLOCK_HEADS, :],
+                    "q",
+                )
+            )
+        blocks.append((Wv, heads_of(v_out), None))
+
+        eps = const.tile([P, 1], F32)
+        nc.vector.memset(eps[:], EPS)
+        warm = const.tile([P, 1], F32)
+        nc.scalar.sqrt(out=warm[:], in_=eps[:])
+
+        ident = const.tile([P, P], F32)
+        make_identity(nc, ident[:])
+        ones = const.tile([P, P], BF16)
+        nc.vector.memset(ones[:], 1.0)
+        vector_rows = const.tile([P, 4 * HEAD], BF16)
+        nc.vector.memset(vector_rows[:], 0.0)
+        for v, vec in enumerate((q_gamma, q_beta, k_gamma, k_beta)):
+            nc.scalar.dma_start(
+                out=vector_rows[0:1, v * HEAD : (v + 1) * HEAD], in_=vec.unsqueeze(0)
+            )
+        cos_sb = const.tile([P, TOKEN_TILES, HEAD], BF16)
+        sin_sb = const.tile([P, TOKEN_TILES, HEAD], BF16)
+        nc.scalar.dma_start(out=cos_sb[:], in_=cos.rearrange("(p i) j -> p i j", i=TOKEN_TILES))
+        nc.scalar.dma_start(out=sin_sb[:], in_=sin.rearrange("(p i) j -> p i j", i=TOKEN_TILES))
+
+        x_sb = const.tile([P, TOKEN_TILES * D_MODEL], BF16)
+        x_rows = x.rearrange("o (p i) k -> p (o i) k", i=TOKEN_TILES)
+        for i in range(TOKEN_TILES):
+            nc.sync.dma_start(out=x_sb[:, i * D_MODEL : (i + 1) * D_MODEL], in_=x_rows[:, i, :])
+
+        raw_tiles = {}
+
+        def load_block(b):
+            rows = blocks[b][0].rearrange("(g p t) n -> g p t n", g=PASSES, t=PACK)
+            for g in range(PASSES):
+                raw = raw_pool.tile([P, PACK, BLOCK], BF16, name="raw")
+                nc.sync.dma_start(out=raw[:], in_=rows[g])
+                raw_tiles[(b, g)] = raw
+
+        for b in range(LOAD_AHEAD):
+            load_block(b)
+
+        spread_ps = psum.tile([P, 4 * HEAD], F32, tag="bank", name="spread_ps")
+        nc.tensor.matmul(out=spread_ps[:], lhsT=ones[:], rhs=vector_rows[:], start=True, stop=True)
+        spread = spread_ps[:].rearrange("p (v j) -> p v j", v=4)
+        signed = const.tile([P, 4, 2, HEAD], F32)
+        nc.scalar.copy(out=signed[:, :, 0, :], in_=spread)
+        nc.scalar.copy(out=signed[:, :, 1, 0:HALF], in_=spread[:, :, 0:HALF])
+        nc.scalar.mul(out=signed[:, :, 1, HALF:HEAD], in_=spread[:, :, HALF:HEAD], mul=-1.0)
+
+        def rotation_products(out, v):
+            def over_tiles(ap):
+                return ap.unsqueeze(1).to_broadcast([P, TOKEN_TILES, ap.shape[1]])
+
+            nc.vector.tensor_tensor(
+                out=out[:, :, 0, :], in0=cos_sb[:], in1=over_tiles(signed[:, v, 0, :]), op=ALU.mult
+            )
+            for lo, partner in ((0, HALF), (HALF, 0)):
+                nc.vector.tensor_tensor(
+                    out=out[:, :, 1, lo : lo + HALF],
+                    in0=sin_sb[:, :, partner : partner + HALF],
+                    in1=over_tiles(signed[:, v, 1, lo : lo + HALF]),
+                    op=ALU.mult,
+                )
+
+        factors = {}
+        shifts = {}
+        for kind, v in (("k", 2), ("q", 0)):
+            factors[kind] = const.tile([P, TOKEN_TILES, 2, HEAD], F32, name="factors_" + kind)
+            rotation_products(factors[kind], v)
+            beta_products = const.tile([P, TOKEN_TILES, 2, HEAD], F32, name="beta_" + kind)
+            rotation_products(beta_products, v + 1)
+            shifts[kind] = const.tile([P, TOKEN_TILES, HEAD], F32, name="shift_" + kind)
+            add_partner_halves(nc, shifts[kind], beta_products)
+
+        x_words = x_sb[:].bitcast(F32).rearrange(
+            "p (i g m u) -> p i g u m", i=TOKEN_TILES, g=PASSES, u=2
+        )
+        x_codes = const.tile([P, TOKEN_TILES, PASSES * P], U32, align_bytes=64)
+        x_scales = const.tile([P, TOKEN_TILES, PASSES * P], U8, align_bytes=64)
+        x_grouped = []
+        for i in range(TOKEN_TILES):
+            grouped = const.tile([P, PASSES * P * PACK], BF16, align_bytes=64, name="x_grouped%d" % i)
+            x_grouped.append(grouped)
+            grouped_words = grouped[:].bitcast(F32).rearrange("p (g s u) -> p g s u", g=PASSES, u=2)
+            for pair in range(PASSES // 2):
+                xt = psum.tile([P, 4 * P], F32, tag="bank", name="xt")
+                for g2 in range(2):
+                    for u in range(2):
+                        nc.tensor.transpose(
+                            xt[:, (2 * g2 + u) * P : (2 * g2 + u + 1) * P],
+                            x_words[:, i, 2 * pair + g2, u, :],
+                            ident[:],
+                        )
+                nc.scalar.copy(
+                    out=grouped_words[:, 2 * pair : 2 * pair + 2, :, :],
+                    in_=xt[:].rearrange("p (g u s) -> p g s u", g=2, u=2),
+                )
+        for i in range(TOKEN_TILES):
+            nc.vector.quantize_mx(
+                out=x_codes[:, i, :].bitcast(FP8X4), scales=x_scales[:, i, :], in_=x_grouped[i][:]
+            )
+
+        unread = const.tile([P, 2 * UNITS, HEAD], BF16)
+        products = const.tile([P, UNITS, 2, HEAD], F32)
+        banks = {}
+        stats = {}
+
+        def head_sums(b, i, h):
+            return banks[(b, i)][:, h * HEAD : (h + 1) * HEAD]
+
+        def regroup(engine_copy, b, g, grouped_tiles):
+            grouped = grouped_pool.tile([P, BLOCK, PACK], BF16, align_bytes=64, name="grouped")
+            engine_copy(
+                out=grouped[:].rearrange("p (c r) t -> p c t r", r=4),
+                in_=raw_tiles[(b, g)][:].rearrange("p t (c r) -> p c t r", r=4),
+            )
+            grouped_tiles[g] = grouped
+
+        for step in range(len(blocks) + 1):
+            fresh, summed, finished = step, step - 1, step - 2
+            has_fresh = fresh < len(blocks)
+            has_summed = 0 <= summed < len(blocks)
+            has_finished = 0 <= finished < len(blocks) and blocks[finished][2] is not None
+            normed = has_summed and blocks[summed][2] is not None
+            vector_copies = VECTOR_COPIES_AT_START if step < 2 else VECTOR_COPIES_LATER
+            scalar_copies = PASSES - vector_copies
+            grouped_tiles = {}
+
+            if has_fresh:
+                regroup(nc.scalar.copy, fresh, 0, grouped_tiles)
+            if normed:
+                sums = stats_pool.tile([P, UNITS], F32, name="sums")
+                for i in range(TOKEN_TILES):
+                    for h in range(BLOCK_HEADS):
+                        unit = h * TOKEN_TILES + i
+                        nc.scalar.activation(
+                            out=unread[:, unit, :],
+                            in_=head_sums(summed, i, h),
+                            func=ACT.Identity,
+                            accum_out=sums[:, unit : unit + 1],
+                        )
+            if has_fresh:
+                for g in range(1, scalar_copies):
+                    regroup(nc.scalar.copy, fresh, g, grouped_tiles)
+            if normed:
+                neg_mean = stats_pool.tile([P, UNITS], F32, name="neg_mean")
+                nc.scalar.mul(out=neg_mean[:], in_=sums[:], mul=-1.0 / HEAD)
+                squares = stats_pool.tile([P, UNITS], F32, name="squares")
+                for i in range(TOKEN_TILES):
+                    for h in range(BLOCK_HEADS):
+                        unit = h * TOKEN_TILES + i
+                        nc.scalar.activation(
+                            out=unread[:, UNITS + unit, :],
+                            in_=head_sums(summed, i, h),
+                            func=ACT.Square,
+                            bias=neg_mean[:, unit : unit + 1],
+                            accum_out=squares[:, unit : unit + 1],
+                        )
+                std = stats_pool.tile([P, UNITS], F32, name="std")
+                nc.scalar.activation(
+                    out=std[:], in_=squares[:], func=ACT.Sqrt, bias=eps[:], scale=1.0 / HEAD
+                )
+                stats[summed] = (neg_mean, std)
+            if has_summed and not normed:
+                values = result_pool.tile([P, UNITS, HEAD], F32, name="result")
+                by_tile = values[:].rearrange("p (h i) j -> p h i j", i=TOKEN_TILES)
+                for i in range(TOKEN_TILES):
+                    nc.scalar.copy(
+                        out=by_tile[:, :, i, :],
+                        in_=banks[(summed, i)][:].rearrange("p (h j) -> p h j", h=BLOCK_HEADS),
+                    )
+                for h in range(BLOCK_HEADS):
+                    nc.sync.dma_start(
+                        out=blocks[summed][1][:, h, :],
+                        in_=values[:, h * TOKEN_TILES : (h + 1) * TOKEN_TILES, :].rearrange(
+                            "p i j -> p (i j)"
+                        ),
+                    )
+
+            if has_fresh:
+                for g in range(scalar_copies, PASSES):
+                    regroup(nc.vector.tensor_copy, fresh, g, grouped_tiles)
+                if fresh + LOAD_AHEAD < len(blocks):
+                    load_block(fresh + LOAD_AHEAD)
+            if has_finished:
+                kind = blocks[finished][2]
+                neg_mean, std = stats[finished]
+                rstd = stats_pool.tile([P, UNITS], F32, name="rstd")
+                nc.vector.reciprocal(out=rstd[:], in_=std[:])
+                for i in range(TOKEN_TILES):
+                    for h in range(BLOCK_HEADS):
+                        unit = h * TOKEN_TILES + i
+                        nc.vector.scalar_tensor_tensor(
+                            out=products[:, unit, :, :],
+                            in0=head_sums(finished, i, h).unsqueeze(1).to_broadcast([P, 2, HEAD]),
+                            scalar=neg_mean[:, unit : unit + 1],
+                            in1=factors[kind][:, i, :, :],
+                            op0=ALU.add,
+                            op1=ALU.mult,
+                        )
+                result = result_pool.tile([P, UNITS, HEAD], F32, name="result")
+                add_partner_halves(nc, result, products)
+                for h in range(BLOCK_HEADS):
+                    for i in range(TOKEN_TILES):
+                        unit = h * TOKEN_TILES + i
+                        nc.vector.scalar_tensor_tensor(
+                            out=result[:, unit, :],
+                            in0=result[:, unit, :],
+                            scalar=rstd[:, unit : unit + 1],
+                            in1=shifts[kind][:, i, :],
+                            op0=ALU.mult,
+                            op1=ALU.add,
+                        )
+                    nc.sync.dma_start(
+                        out=blocks[finished][1][:, h, :],
+                        in_=result[:, h * TOKEN_TILES : (h + 1) * TOKEN_TILES, :].rearrange(
+                            "p i j -> p (i j)"
+                        ),
+                    )
+            if has_fresh:
+                w_codes = codes_pool.tile([P, PASSES, BLOCK], U32, align_bytes=64, name="w_codes")
+                w_scales = codes_pool.tile([P, PASSES, BLOCK], U8, align_bytes=64, name="w_scales")
+                for g in range(PASSES):
+                    nc.vector.quantize_mx(
+                        out=w_codes[:, g, :].bitcast(FP8X4),
+                        scales=w_scales[:, g, :],
+                        in_=grouped_tiles[g][:].rearrange("p n t -> p (n t)"),
+                    )
+                for i in range(TOKEN_TILES):
+                    bank = psum.tile([P, BLOCK], F32, tag="bank", name="bank")
+                    banks[(fresh, i)] = bank
+                    for g in range(PASSES):
+                        nc.tensor.matmul_mx(
+                            out=bank[:],
+                            lhsT=x_codes[:, i, g * P : (g + 1) * P].bitcast(FP8X4),
+                            lhsT_scale=x_scales[:, i, g * P : (g + 1) * P],
+                            rhs=w_codes[:, g, :].bitcast(FP8X4),
+                            rhs_scale=w_scales[:, g, :],
+                            start=(g == 0),
+                            stop=(g == PASSES - 1),
+                        )

@@ -26,15 +26,14 @@ UNITS = BLOCK_HEADS * TOKEN_TILES
 Q_BLOCKS = 4
 EPS = 1e-6
 LOAD_AHEAD = 3
-VECTOR_COPIES_AT_START = 2
-VECTOR_COPIES_LATER = 1
+SCALAR_COPIES = 2
 
 FLOPS = 2 * TOKENS * D_MODEL * (Q_BLOCKS + 2) * BLOCK
 
 
-def add_partner_halves(nc, out, products):
+def add_partner_halves(engine, out, products):
     for lo, partner in ((0, HALF), (HALF, 0)):
-        nc.vector.tensor_tensor(
+        engine.tensor_tensor(
             out=out[:, :, lo : lo + HALF],
             in0=products[:, :, 0, lo : lo + HALF],
             in1=products[:, :, 1, partner : partner + HALF],
@@ -52,8 +51,7 @@ def tile_gqa_flashattn_pa_kernel(
         raw_pool = ctx.enter_context(tc.tile_pool(name="raw", bufs=LOAD_AHEAD * PASSES))
         grouped_pool = ctx.enter_context(tc.tile_pool(name="grouped", bufs=2 * PASSES))
         codes_pool = ctx.enter_context(tc.tile_pool(name="codes", bufs=2))
-        stats_pool = ctx.enter_context(tc.tile_pool(name="stats", bufs=3))
-        result_pool = ctx.enter_context(tc.tile_pool(name="result", bufs=2))
+        stats_pool = ctx.enter_context(tc.tile_pool(name="stats", bufs=4))
         psum = ctx.enter_context(tc.psum_pool(name="psum", bufs=8))
 
         def heads_of(out):
@@ -70,6 +68,14 @@ def tile_gqa_flashattn_pa_kernel(
             )
         blocks.append((Wv, heads_of(v_out), None))
 
+        def store_head(b, h, result):
+            nc.sync.dma_start(
+                out=blocks[b][1][:, h, :],
+                in_=result[:, h * TOKEN_TILES : (h + 1) * TOKEN_TILES, :].rearrange(
+                    "p i j -> p (i j)"
+                ),
+            )
+
         eps = const.tile([P, 1], F32)
         nc.vector.memset(eps[:], EPS)
         warm = const.tile([P, 1], F32)
@@ -82,18 +88,13 @@ def tile_gqa_flashattn_pa_kernel(
         vector_rows = const.tile([P, 4 * HEAD], BF16)
         nc.vector.memset(vector_rows[:], 0.0)
         for v, vec in enumerate((q_gamma, q_beta, k_gamma, k_beta)):
-            nc.scalar.dma_start(
+            nc.sync.dma_start(
                 out=vector_rows[0:1, v * HEAD : (v + 1) * HEAD], in_=vec.unsqueeze(0)
             )
         cos_sb = const.tile([P, TOKEN_TILES, HEAD], BF16)
         sin_sb = const.tile([P, TOKEN_TILES, HEAD], BF16)
-        nc.scalar.dma_start(out=cos_sb[:], in_=cos.rearrange("(p i) j -> p i j", i=TOKEN_TILES))
-        nc.scalar.dma_start(out=sin_sb[:], in_=sin.rearrange("(p i) j -> p i j", i=TOKEN_TILES))
-
-        x_sb = const.tile([P, TOKEN_TILES * D_MODEL], BF16)
-        x_rows = x.rearrange("o (p i) k -> p (o i) k", i=TOKEN_TILES)
-        for i in range(TOKEN_TILES):
-            nc.sync.dma_start(out=x_sb[:, i * D_MODEL : (i + 1) * D_MODEL], in_=x_rows[:, i, :])
+        nc.sync.dma_start(out=cos_sb[:], in_=cos.rearrange("(p i) j -> p i j", i=TOKEN_TILES))
+        nc.sync.dma_start(out=sin_sb[:], in_=sin.rearrange("(p i) j -> p i j", i=TOKEN_TILES))
 
         raw_tiles = {}
 
@@ -104,74 +105,97 @@ def tile_gqa_flashattn_pa_kernel(
                 nc.sync.dma_start(out=raw[:], in_=rows[g])
                 raw_tiles[(b, g)] = raw
 
-        for b in range(LOAD_AHEAD):
-            load_block(b)
-
-        spread_ps = psum.tile([P, 4 * HEAD], F32, tag="bank", name="spread_ps")
-        nc.tensor.matmul(out=spread_ps[:], lhsT=ones[:], rhs=vector_rows[:], start=True, stop=True)
-        spread = spread_ps[:].rearrange("p (v j) -> p v j", v=4)
         signed = const.tile([P, 4, 2, HEAD], F32)
-        nc.scalar.copy(out=signed[:, :, 0, :], in_=spread)
-        nc.scalar.copy(out=signed[:, :, 1, 0:HALF], in_=spread[:, :, 0:HALF])
-        nc.scalar.mul(out=signed[:, :, 1, HALF:HEAD], in_=spread[:, :, HALF:HEAD], mul=-1.0)
-
-        def rotation_products(out, v):
-            def over_tiles(ap):
-                return ap.unsqueeze(1).to_broadcast([P, TOKEN_TILES, ap.shape[1]])
-
-            nc.vector.tensor_tensor(
-                out=out[:, :, 0, :], in0=cos_sb[:], in1=over_tiles(signed[:, v, 0, :]), op=ALU.mult
-            )
-            for lo, partner in ((0, HALF), (HALF, 0)):
-                nc.vector.tensor_tensor(
-                    out=out[:, :, 1, lo : lo + HALF],
-                    in0=sin_sb[:, :, partner : partner + HALF],
-                    in1=over_tiles(signed[:, v, 1, lo : lo + HALF]),
-                    op=ALU.mult,
-                )
-
         factors = {}
         shifts = {}
-        for kind, v in (("k", 2), ("q", 0)):
+        for kind in ("k", "q"):
             factors[kind] = const.tile([P, TOKEN_TILES, 2, HEAD], F32, name="factors_" + kind)
-            rotation_products(factors[kind], v)
-            beta_products = const.tile([P, TOKEN_TILES, 2, HEAD], F32, name="beta_" + kind)
-            rotation_products(beta_products, v + 1)
             shifts[kind] = const.tile([P, TOKEN_TILES, HEAD], F32, name="shift_" + kind)
-            add_partner_halves(nc, shifts[kind], beta_products)
-
-        x_words = x_sb[:].bitcast(F32).rearrange(
-            "p (i g m u) -> p i g u m", i=TOKEN_TILES, g=PASSES, u=2
-        )
         x_codes = const.tile([P, TOKEN_TILES, PASSES * P], U32, align_bytes=64)
         x_scales = const.tile([P, TOKEN_TILES, PASSES * P], U8, align_bytes=64)
-        x_grouped = []
-        for i in range(TOKEN_TILES):
-            grouped = const.tile([P, PASSES * P * PACK], BF16, align_bytes=64, name="x_grouped%d" % i)
-            x_grouped.append(grouped)
-            grouped_words = grouped[:].bitcast(F32).rearrange("p (g s u) -> p g s u", g=PASSES, u=2)
-            for pair in range(PASSES // 2):
-                xt = psum.tile([P, 4 * P], F32, tag="bank", name="xt")
-                for g2 in range(2):
-                    for u in range(2):
-                        nc.tensor.transpose(
-                            xt[:, (2 * g2 + u) * P : (2 * g2 + u + 1) * P],
-                            x_words[:, i, 2 * pair + g2, u, :],
-                            ident[:],
-                        )
-                nc.scalar.copy(
-                    out=grouped_words[:, 2 * pair : 2 * pair + 2, :, :],
-                    in_=xt[:].rearrange("p (g u s) -> p g s u", g=2, u=2),
-                )
-        for i in range(TOKEN_TILES):
-            nc.vector.quantize_mx(
-                out=x_codes[:, i, :].bitcast(FP8X4), scales=x_scales[:, i, :], in_=x_grouped[i][:]
-            )
 
-        unread = const.tile([P, 2 * UNITS, HEAD], BF16)
-        products = const.tile([P, UNITS, 2, HEAD], F32)
+        with tc.tile_pool(name="stage", bufs=1) as stage:
+            x_sb = stage.tile([P, TOKEN_TILES * D_MODEL], BF16)
+            x_rows = x.rearrange("o (p i) k -> p (o i) k", i=TOKEN_TILES)
+            for i in range(TOKEN_TILES):
+                nc.sync.dma_start(
+                    out=x_sb[:, i * D_MODEL : (i + 1) * D_MODEL], in_=x_rows[:, i, :]
+                )
+            for b in range(LOAD_AHEAD):
+                load_block(b)
+
+            spread_ps = psum.tile([P, 4 * HEAD], F32, tag="bank", name="spread_ps")
+            nc.tensor.matmul(
+                out=spread_ps[:], lhsT=ones[:], rhs=vector_rows[:], start=True, stop=True
+            )
+            spread = spread_ps[:].rearrange("p (v j) -> p v j", v=4)
+            nc.scalar.copy(out=signed[:, :, 0, :], in_=spread)
+            nc.scalar.copy(out=signed[:, :, 1, 0:HALF], in_=spread[:, :, 0:HALF])
+            nc.scalar.mul(out=signed[:, :, 1, HALF:HEAD], in_=spread[:, :, HALF:HEAD], mul=-1.0)
+
+            def rotation_products(out, v):
+                def over_tiles(ap):
+                    return ap.unsqueeze(1).to_broadcast([P, TOKEN_TILES, ap.shape[1]])
+
+                nc.vector.tensor_tensor(
+                    out=out[:, :, 0, :],
+                    in0=cos_sb[:],
+                    in1=over_tiles(signed[:, v, 0, :]),
+                    op=ALU.mult,
+                )
+                for lo, partner in ((0, HALF), (HALF, 0)):
+                    nc.vector.tensor_tensor(
+                        out=out[:, :, 1, lo : lo + HALF],
+                        in0=sin_sb[:, :, partner : partner + HALF],
+                        in1=over_tiles(signed[:, v, 1, lo : lo + HALF]),
+                        op=ALU.mult,
+                    )
+
+            for kind, v in (("k", 2), ("q", 0)):
+                rotation_products(factors[kind], v)
+                beta_products = stage.tile([P, TOKEN_TILES, 2, HEAD], F32, name="beta_" + kind)
+                rotation_products(beta_products, v + 1)
+                add_partner_halves(nc.vector, shifts[kind], beta_products)
+
+            x_words = x_sb[:].bitcast(F32).rearrange(
+                "p (i g m u) -> p i g u m", i=TOKEN_TILES, g=PASSES, u=2
+            )
+            x_grouped = []
+            for i in range(TOKEN_TILES):
+                grouped = stage.tile(
+                    [P, PASSES * P * PACK], BF16, align_bytes=64, name="x_grouped%d" % i
+                )
+                x_grouped.append(grouped)
+                grouped_words = grouped[:].bitcast(F32).rearrange(
+                    "p (g s u) -> p g s u", g=PASSES, u=2
+                )
+                for pair in range(PASSES // 2):
+                    xt = psum.tile([P, 4 * P], F32, tag="bank", name="xt")
+                    for g2 in range(2):
+                        for u in range(2):
+                            nc.tensor.transpose(
+                                xt[:, (2 * g2 + u) * P : (2 * g2 + u + 1) * P],
+                                x_words[:, i, 2 * pair + g2, u, :],
+                                ident[:],
+                            )
+                    nc.scalar.copy(
+                        out=grouped_words[:, 2 * pair : 2 * pair + 2, :, :],
+                        in_=xt[:].rearrange("p (g u s) -> p g s u", g=2, u=2),
+                    )
+            for i in range(TOKEN_TILES):
+                nc.vector.quantize_mx(
+                    out=x_codes[:, i, :].bitcast(FP8X4),
+                    scales=x_scales[:, i, :],
+                    in_=x_grouped[i][:],
+                )
+
+        late = ctx.enter_context(tc.tile_pool(name="late", bufs=1))
+        products_pool = ctx.enter_context(tc.tile_pool(name="products", bufs=2))
+        result_pool = ctx.enter_context(tc.tile_pool(name="result", bufs=3))
+        unread = late.tile([P, 2 * UNITS, HEAD], BF16)
         banks = {}
         stats = {}
+        rotated = {}
 
         def head_sums(b, i, h):
             return banks[(b, i)][:, h * HEAD : (h + 1) * HEAD]
@@ -184,19 +208,17 @@ def tile_gqa_flashattn_pa_kernel(
             )
             grouped_tiles[g] = grouped
 
-        for step in range(len(blocks) + 1):
-            fresh, summed, finished = step, step - 1, step - 2
+        def has_norm(b):
+            return 0 <= b < len(blocks) and blocks[b][2] is not None
+
+        for step in range(len(blocks) + 2):
+            fresh, summed, centred, scaled = step, step - 1, step - 2, step - 3
             has_fresh = fresh < len(blocks)
-            has_summed = 0 <= summed < len(blocks)
-            has_finished = 0 <= finished < len(blocks) and blocks[finished][2] is not None
-            normed = has_summed and blocks[summed][2] is not None
-            vector_copies = VECTOR_COPIES_AT_START if step < 2 else VECTOR_COPIES_LATER
-            scalar_copies = PASSES - vector_copies
             grouped_tiles = {}
 
             if has_fresh:
                 regroup(nc.scalar.copy, fresh, 0, grouped_tiles)
-            if normed:
+            if has_norm(summed):
                 sums = stats_pool.tile([P, UNITS], F32, name="sums")
                 for i in range(TOKEN_TILES):
                     for h in range(BLOCK_HEADS):
@@ -208,9 +230,9 @@ def tile_gqa_flashattn_pa_kernel(
                             accum_out=sums[:, unit : unit + 1],
                         )
             if has_fresh:
-                for g in range(1, scalar_copies):
+                for g in range(1, SCALAR_COPIES):
                     regroup(nc.scalar.copy, fresh, g, grouped_tiles)
-            if normed:
+            if has_norm(summed):
                 neg_mean = stats_pool.tile([P, UNITS], F32, name="neg_mean")
                 nc.scalar.mul(out=neg_mean[:], in_=sums[:], mul=-1.0 / HEAD)
                 squares = stats_pool.tile([P, UNITS], F32, name="squares")
@@ -229,7 +251,7 @@ def tile_gqa_flashattn_pa_kernel(
                     out=std[:], in_=squares[:], func=ACT.Sqrt, bias=eps[:], scale=1.0 / HEAD
                 )
                 stats[summed] = (neg_mean, std)
-            if has_summed and not normed:
+            if summed == len(blocks) - 1:
                 values = result_pool.tile([P, UNITS, HEAD], F32, name="result")
                 by_tile = values[:].rearrange("p (h i) j -> p h i j", i=TOKEN_TILES)
                 for i in range(TOKEN_TILES):
@@ -238,36 +260,35 @@ def tile_gqa_flashattn_pa_kernel(
                         in_=banks[(summed, i)][:].rearrange("p (h j) -> p h j", h=BLOCK_HEADS),
                     )
                 for h in range(BLOCK_HEADS):
-                    nc.sync.dma_start(
-                        out=blocks[summed][1][:, h, :],
-                        in_=values[:, h * TOKEN_TILES : (h + 1) * TOKEN_TILES, :].rearrange(
-                            "p i j -> p (i j)"
-                        ),
-                    )
+                    store_head(summed, h, values)
 
             if has_fresh:
-                for g in range(scalar_copies, PASSES):
+                for g in range(SCALAR_COPIES, PASSES):
                     regroup(nc.vector.tensor_copy, fresh, g, grouped_tiles)
                 if fresh + LOAD_AHEAD < len(blocks):
                     load_block(fresh + LOAD_AHEAD)
-            if has_finished:
-                kind = blocks[finished][2]
-                neg_mean, std = stats[finished]
+            if has_norm(centred):
+                neg_mean, std = stats[centred]
                 rstd = stats_pool.tile([P, UNITS], F32, name="rstd")
                 nc.vector.reciprocal(out=rstd[:], in_=std[:])
-                for i in range(TOKEN_TILES):
-                    for h in range(BLOCK_HEADS):
+                products = products_pool.tile([P, UNITS, 2, HEAD], F32, name="products")
+                result = result_pool.tile([P, UNITS, HEAD], F32, name="result")
+                for h in range(BLOCK_HEADS):
+                    for i in range(TOKEN_TILES):
                         unit = h * TOKEN_TILES + i
                         nc.vector.scalar_tensor_tensor(
                             out=products[:, unit, :, :],
-                            in0=head_sums(finished, i, h).unsqueeze(1).to_broadcast([P, 2, HEAD]),
+                            in0=head_sums(centred, i, h).unsqueeze(1).to_broadcast([P, 2, HEAD]),
                             scalar=neg_mean[:, unit : unit + 1],
-                            in1=factors[kind][:, i, :, :],
+                            in1=factors[blocks[centred][2]][:, i, :, :],
                             op0=ALU.add,
                             op1=ALU.mult,
                         )
-                result = result_pool.tile([P, UNITS, HEAD], F32, name="result")
-                add_partner_halves(nc, result, products)
+                    units = slice(h * TOKEN_TILES, (h + 1) * TOKEN_TILES)
+                    add_partner_halves(nc.gpsimd, result[:, units, :], products[:, units, :, :])
+                rotated[centred] = (rstd, result)
+            if has_norm(scaled):
+                rstd, result = rotated[scaled]
                 for h in range(BLOCK_HEADS):
                     for i in range(TOKEN_TILES):
                         unit = h * TOKEN_TILES + i
@@ -275,16 +296,11 @@ def tile_gqa_flashattn_pa_kernel(
                             out=result[:, unit, :],
                             in0=result[:, unit, :],
                             scalar=rstd[:, unit : unit + 1],
-                            in1=shifts[kind][:, i, :],
+                            in1=shifts[blocks[scaled][2]][:, i, :],
                             op0=ALU.mult,
                             op1=ALU.add,
                         )
-                    nc.sync.dma_start(
-                        out=blocks[finished][1][:, h, :],
-                        in_=result[:, h * TOKEN_TILES : (h + 1) * TOKEN_TILES, :].rearrange(
-                            "p i j -> p (i j)"
-                        ),
-                    )
+                    store_head(scaled, h, result)
             if has_fresh:
                 w_codes = codes_pool.tile([P, PASSES, BLOCK], U32, align_bytes=64, name="w_codes")
                 w_scales = codes_pool.tile([P, PASSES, BLOCK], U8, align_bytes=64, name="w_scales")

@@ -25,7 +25,7 @@ BLOCK = BLOCK_HEADS * HEAD
 UNITS = BLOCK_HEADS * TOKEN_TILES
 Q_BLOCKS = 4
 EPS = 1e-6
-LOAD_AHEAD = 3
+AHEAD = 3
 SCALAR_COPIES = 2
 
 FLOPS = 2 * TOKENS * D_MODEL * (Q_BLOCKS + 2) * BLOCK
@@ -48,9 +48,9 @@ def tile_gqa_flashattn_pa_kernel(
     with ExitStack() as ctx:
         ctx.enter_context(tc.manual_schedule())
         const = ctx.enter_context(tc.tile_pool(name="const", bufs=1))
-        raw_pool = ctx.enter_context(tc.tile_pool(name="raw", bufs=LOAD_AHEAD * PASSES))
+        raw_pool = ctx.enter_context(tc.tile_pool(name="raw", bufs=AHEAD * PASSES))
         grouped_pool = ctx.enter_context(tc.tile_pool(name="grouped", bufs=2 * PASSES))
-        codes_pool = ctx.enter_context(tc.tile_pool(name="codes", bufs=2))
+        codes_pool = ctx.enter_context(tc.tile_pool(name="codes", bufs=AHEAD))
         stats_pool = ctx.enter_context(tc.tile_pool(name="stats", bufs=4))
         psum = ctx.enter_context(tc.psum_pool(name="psum", bufs=8))
 
@@ -121,7 +121,7 @@ def tile_gqa_flashattn_pa_kernel(
                 nc.sync.dma_start(
                     out=x_sb[:, i * D_MODEL : (i + 1) * D_MODEL], in_=x_rows[:, i, :]
                 )
-            for b in range(LOAD_AHEAD):
+            for b in range(AHEAD):
                 load_block(b)
 
             spread_ps = psum.tile([P, 4 * HEAD], F32, tag="bank", name="spread_ps")
@@ -200,24 +200,51 @@ def tile_gqa_flashattn_pa_kernel(
         def head_sums(b, i, h):
             return banks[(b, i)][:, h * HEAD : (h + 1) * HEAD]
 
-        def regroup(engine_copy, b, g, grouped_tiles):
+        grouped_tiles = {}
+        codes = {}
+
+        def regroup(engine_copy, b, g):
             grouped = grouped_pool.tile([P, BLOCK, PACK], BF16, align_bytes=64, name="grouped")
             engine_copy(
                 out=grouped[:].rearrange("p (c r) t -> p c t r", r=4),
                 in_=raw_tiles[(b, g)][:].rearrange("p t (c r) -> p c t r", r=4),
             )
-            grouped_tiles[g] = grouped
+            grouped_tiles[(b, g)] = grouped
 
         def has_norm(b):
             return 0 <= b < len(blocks) and blocks[b][2] is not None
 
-        for step in range(len(blocks) + 2):
-            fresh, summed, centred, scaled = step, step - 1, step - 2, step - 3
-            has_fresh = fresh < len(blocks)
-            grouped_tiles = {}
+        def quantise(b):
+            w_codes = codes_pool.tile([P, PASSES, BLOCK], U32, align_bytes=64, name="w_codes")
+            w_scales = codes_pool.tile([P, PASSES, BLOCK], U8, align_bytes=64, name="w_scales")
+            for g in range(PASSES):
+                nc.vector.quantize_mx(
+                    out=w_codes[:, g, :].bitcast(FP8X4),
+                    scales=w_scales[:, g, :],
+                    in_=grouped_tiles[(b, g)][:].rearrange("p n t -> p (n t)"),
+                )
+            codes[b] = (w_codes, w_scales)
 
+        def multiply(b):
+            w_codes, w_scales = codes[b]
+            for i in range(TOKEN_TILES):
+                bank = psum.tile([P, BLOCK], F32, tag="bank", name="bank")
+                banks[(b, i)] = bank
+                for g in range(PASSES):
+                    nc.tensor.matmul_mx(
+                        out=bank[:],
+                        lhsT=x_codes[:, i, g * P : (g + 1) * P].bitcast(FP8X4),
+                        lhsT_scale=x_scales[:, i, g * P : (g + 1) * P],
+                        rhs=w_codes[:, g, :].bitcast(FP8X4),
+                        rhs_scale=w_scales[:, g, :],
+                        start=(g == 0),
+                        stop=(g == PASSES - 1),
+                    )
+
+        def scalar_work(summed, fresh):
+            has_fresh = fresh < len(blocks)
             if has_fresh:
-                regroup(nc.scalar.copy, fresh, 0, grouped_tiles)
+                regroup(nc.scalar.copy, fresh, 0)
             if has_norm(summed):
                 sums = stats_pool.tile([P, UNITS], F32, name="sums")
                 for i in range(TOKEN_TILES):
@@ -231,7 +258,7 @@ def tile_gqa_flashattn_pa_kernel(
                         )
             if has_fresh:
                 for g in range(1, SCALAR_COPIES):
-                    regroup(nc.scalar.copy, fresh, g, grouped_tiles)
+                    regroup(nc.scalar.copy, fresh, g)
             if has_norm(summed):
                 neg_mean = stats_pool.tile([P, UNITS], F32, name="neg_mean")
                 nc.scalar.mul(out=neg_mean[:], in_=sums[:], mul=-1.0 / HEAD)
@@ -262,33 +289,45 @@ def tile_gqa_flashattn_pa_kernel(
                 for h in range(BLOCK_HEADS):
                     store_head(summed, h, values)
 
-            if has_fresh:
-                for g in range(SCALAR_COPIES, PASSES):
-                    regroup(nc.vector.tensor_copy, fresh, g, grouped_tiles)
-                if fresh + LOAD_AHEAD < len(blocks):
-                    load_block(fresh + LOAD_AHEAD)
-            if has_norm(centred):
-                neg_mean, std = stats[centred]
+        def vector_prepare(fresh):
+            for g in range(SCALAR_COPIES, PASSES):
+                regroup(nc.vector.tensor_copy, fresh, g)
+            if fresh + AHEAD < len(blocks):
+                load_block(fresh + AHEAD)
+            quantise(fresh)
+
+        for b in range(AHEAD):
+            scalar_work(-1, b)
+            vector_prepare(b)
+            if b < 2:
+                multiply(b)
+        scalar_work(0, len(blocks))
+
+        for b in range(len(blocks)):
+            scalar_work(b + 1, b + AHEAD)
+            if has_norm(b):
+                neg_mean, std = stats[b]
                 rstd = stats_pool.tile([P, UNITS], F32, name="rstd")
                 nc.vector.reciprocal(out=rstd[:], in_=std[:])
                 products = products_pool.tile([P, UNITS, 2, HEAD], F32, name="products")
-                result = result_pool.tile([P, UNITS, HEAD], F32, name="result")
-                for h in range(BLOCK_HEADS):
-                    for i in range(TOKEN_TILES):
+                for i in range(TOKEN_TILES):
+                    for h in range(BLOCK_HEADS):
                         unit = h * TOKEN_TILES + i
                         nc.vector.scalar_tensor_tensor(
                             out=products[:, unit, :, :],
-                            in0=head_sums(centred, i, h).unsqueeze(1).to_broadcast([P, 2, HEAD]),
+                            in0=head_sums(b, i, h).unsqueeze(1).to_broadcast([P, 2, HEAD]),
                             scalar=neg_mean[:, unit : unit + 1],
-                            in1=factors[blocks[centred][2]][:, i, :, :],
+                            in1=factors[blocks[b][2]][:, i, :, :],
                             op0=ALU.add,
                             op1=ALU.mult,
                         )
-                    units = slice(h * TOKEN_TILES, (h + 1) * TOKEN_TILES)
-                    add_partner_halves(nc.gpsimd, result[:, units, :], products[:, units, :, :])
-                rotated[centred] = (rstd, result)
-            if has_norm(scaled):
-                rstd, result = rotated[scaled]
+                result = result_pool.tile([P, UNITS, HEAD], F32, name="result")
+                add_partner_halves(nc.gpsimd, result, products)
+                rotated[b] = (rstd, result)
+            if b + 2 < len(blocks):
+                multiply(b + 2)
+            if has_norm(b - 1):
+                rstd, result = rotated[b - 1]
                 for h in range(BLOCK_HEADS):
                     for i in range(TOKEN_TILES):
                         unit = h * TOKEN_TILES + i
@@ -296,30 +335,10 @@ def tile_gqa_flashattn_pa_kernel(
                             out=result[:, unit, :],
                             in0=result[:, unit, :],
                             scalar=rstd[:, unit : unit + 1],
-                            in1=shifts[blocks[scaled][2]][:, i, :],
+                            in1=shifts[blocks[b - 1][2]][:, i, :],
                             op0=ALU.mult,
                             op1=ALU.add,
                         )
-                    store_head(scaled, h, result)
-            if has_fresh:
-                w_codes = codes_pool.tile([P, PASSES, BLOCK], U32, align_bytes=64, name="w_codes")
-                w_scales = codes_pool.tile([P, PASSES, BLOCK], U8, align_bytes=64, name="w_scales")
-                for g in range(PASSES):
-                    nc.vector.quantize_mx(
-                        out=w_codes[:, g, :].bitcast(FP8X4),
-                        scales=w_scales[:, g, :],
-                        in_=grouped_tiles[g][:].rearrange("p n t -> p (n t)"),
-                    )
-                for i in range(TOKEN_TILES):
-                    bank = psum.tile([P, BLOCK], F32, tag="bank", name="bank")
-                    banks[(fresh, i)] = bank
-                    for g in range(PASSES):
-                        nc.tensor.matmul_mx(
-                            out=bank[:],
-                            lhsT=x_codes[:, i, g * P : (g + 1) * P].bitcast(FP8X4),
-                            lhsT_scale=x_scales[:, i, g * P : (g + 1) * P],
-                            rhs=w_codes[:, g, :].bitcast(FP8X4),
-                            rhs_scale=w_scales[:, g, :],
-                            start=(g == 0),
-                            stop=(g == PASSES - 1),
-                        )
+                    store_head(b - 1, h, result)
+            if b + AHEAD < len(blocks):
+                vector_prepare(b + AHEAD)

@@ -105,7 +105,6 @@ def tile_gqa_flashattn_pa_kernel(
                 nc.sync.dma_start(out=raw[:], in_=rows[g])
                 raw_tiles[(b, g)] = raw
 
-        signed = const.tile([P, 4, 2, HEAD], F32)
         factors = {}
         shifts = {}
         for kind in ("k", "q"):
@@ -129,26 +128,22 @@ def tile_gqa_flashattn_pa_kernel(
                 out=spread_ps[:], lhsT=ones[:], rhs=vector_rows[:], start=True, stop=True
             )
             spread = spread_ps[:].rearrange("p (v j) -> p v j", v=4)
-            nc.scalar.copy(out=signed[:, :, 0, :], in_=spread)
-            nc.scalar.copy(out=signed[:, :, 1, 0:HALF], in_=spread[:, :, 0:HALF])
-            nc.scalar.mul(out=signed[:, :, 1, HALF:HEAD], in_=spread[:, :, HALF:HEAD], mul=-1.0)
 
             def rotation_products(out, v):
                 def over_tiles(ap):
                     return ap.unsqueeze(1).to_broadcast([P, TOKEN_TILES, ap.shape[1]])
 
                 nc.vector.tensor_tensor(
-                    out=out[:, :, 0, :],
-                    in0=cos_sb[:],
-                    in1=over_tiles(signed[:, v, 0, :]),
-                    op=ALU.mult,
+                    out=out[:, :, 0, :], in0=cos_sb[:], in1=over_tiles(spread[:, v, :]), op=ALU.mult
                 )
-                for lo, partner in ((0, HALF), (HALF, 0)):
-                    nc.vector.tensor_tensor(
+                for lo, partner, sign in ((0, HALF, 1.0), (HALF, 0, -1.0)):
+                    nc.vector.scalar_tensor_tensor(
                         out=out[:, :, 1, lo : lo + HALF],
                         in0=sin_sb[:, :, partner : partner + HALF],
-                        in1=over_tiles(signed[:, v, 1, lo : lo + HALF]),
-                        op=ALU.mult,
+                        scalar=sign,
+                        in1=over_tiles(spread[:, v, lo : lo + HALF]),
+                        op0=ALU.mult,
+                        op1=ALU.mult,
                     )
 
             for kind, v in (("k", 2), ("q", 0)):
@@ -241,10 +236,15 @@ def tile_gqa_flashattn_pa_kernel(
                         stop=(g == PASSES - 1),
                     )
 
+        def scalar_copies_of(b):
+            if b >= len(blocks) or b == AHEAD - 1:
+                return 0
+            return SCALAR_COPIES
+
         def scalar_work(summed, fresh):
-            has_fresh = fresh < len(blocks)
-            if has_fresh:
-                regroup(nc.scalar.copy, fresh, 0)
+            copies = list(range(scalar_copies_of(fresh)))
+            for g in copies[:1]:
+                regroup(nc.scalar.copy, fresh, g)
             if has_norm(summed):
                 sums = stats_pool.tile([P, UNITS], F32, name="sums")
                 for i in range(TOKEN_TILES):
@@ -256,9 +256,8 @@ def tile_gqa_flashattn_pa_kernel(
                             func=ACT.Identity,
                             accum_out=sums[:, unit : unit + 1],
                         )
-            if has_fresh:
-                for g in range(1, SCALAR_COPIES):
-                    regroup(nc.scalar.copy, fresh, g)
+            for g in copies[1:]:
+                regroup(nc.scalar.copy, fresh, g)
             if has_norm(summed):
                 neg_mean = stats_pool.tile([P, UNITS], F32, name="neg_mean")
                 nc.scalar.mul(out=neg_mean[:], in_=sums[:], mul=-1.0 / HEAD)
@@ -290,7 +289,7 @@ def tile_gqa_flashattn_pa_kernel(
                     store_head(summed, h, values)
 
         def vector_prepare(fresh):
-            for g in range(SCALAR_COPIES, PASSES):
+            for g in range(scalar_copies_of(fresh), PASSES):
                 regroup(nc.vector.tensor_copy, fresh, g)
             if fresh + AHEAD < len(blocks):
                 load_block(fresh + AHEAD)

@@ -26,7 +26,12 @@ UNITS = BLOCK_HEADS * TOKEN_TILES
 Q_BLOCKS = 4
 EPS = 1e-6
 AHEAD = 3
-SCALAR_COPIES = 2
+ROUTES = ("TTVV", "TSVV", "SVVV", "TTSV", "TTSV", "TTSV")
+
+
+def TAIL_ENGINE(nc, more):
+    return nc.gpsimd if more else nc.vector
+
 
 FLOPS = 2 * TOKENS * D_MODEL * (Q_BLOCKS + 2) * BLOCK
 
@@ -52,7 +57,10 @@ def tile_gqa_flashattn_pa_kernel(
         grouped_pool = ctx.enter_context(tc.tile_pool(name="grouped", bufs=2 * PASSES))
         codes_pool = ctx.enter_context(tc.tile_pool(name="codes", bufs=AHEAD))
         stats_pool = ctx.enter_context(tc.tile_pool(name="stats", bufs=4))
-        psum = ctx.enter_context(tc.psum_pool(name="psum", bufs=8))
+        psum_pools = (
+            ctx.enter_context(tc.psum_pool(name="psum_even", bufs=TOKEN_TILES)),
+            ctx.enter_context(tc.psum_pool(name="psum_odd", bufs=TOKEN_TILES)),
+        )
 
         def heads_of(out):
             return out.rearrange("o h (p i) j -> p (o h) (i j)", i=TOKEN_TILES)
@@ -83,6 +91,8 @@ def tile_gqa_flashattn_pa_kernel(
 
         ident = const.tile([P, P], F32)
         make_identity(nc, ident[:])
+        ident_bf = const.tile([P, P], BF16)
+        make_identity(nc, ident_bf[:])
         ones = const.tile([P, P], BF16)
         nc.vector.memset(ones[:], 1.0)
         vector_rows = const.tile([P, 4 * HEAD], BF16)
@@ -123,7 +133,7 @@ def tile_gqa_flashattn_pa_kernel(
             for b in range(AHEAD):
                 load_block(b)
 
-            spread_ps = psum.tile([P, 4 * HEAD], F32, tag="bank", name="spread_ps")
+            spread_ps = psum_pools[0].tile([P, 4 * HEAD], F32, tag="bank", name="spread_ps")
             nc.tensor.matmul(
                 out=spread_ps[:], lhsT=ones[:], rhs=vector_rows[:], start=True, stop=True
             )
@@ -165,7 +175,7 @@ def tile_gqa_flashattn_pa_kernel(
                     "p (g s u) -> p g s u", g=PASSES, u=2
                 )
                 for pair in range(PASSES // 2):
-                    xt = psum.tile([P, 4 * P], F32, tag="bank", name="xt")
+                    xt = psum_pools[1].tile([P, 4 * P], F32, tag="bank", name="xt")
                     for g2 in range(2):
                         for u in range(2):
                             nc.tensor.transpose(
@@ -189,6 +199,7 @@ def tile_gqa_flashattn_pa_kernel(
         result_pool = ctx.enter_context(tc.tile_pool(name="result", bufs=3))
         unread = late.tile([P, 2 * UNITS, HEAD], BF16)
         banks = {}
+        neg_means = {}
         stats = {}
         rotated = {}
 
@@ -206,13 +217,41 @@ def tile_gqa_flashattn_pa_kernel(
             )
             grouped_tiles[(b, g)] = grouped
 
+        def regroup_on_tensor(pool, b, g):
+            grouped = grouped_pool.tile([P, BLOCK, PACK], BF16, align_bytes=64, name="grouped")
+            flat = grouped[:].rearrange("p n t -> p (n t)")
+            raw = raw_tiles[(b, g)]
+            for half in range(2):
+                mixed = pool.tile([P, 2 * BLOCK], BF16, tag="bank", name="mixed")
+                for q in range(2):
+                    c0 = (2 * half + q) * P
+                    nc.tensor.matmul(
+                        out=mixed[:, q * BLOCK : (q + 1) * BLOCK].rearrange(
+                            "p (c t) -> p c t", t=PACK
+                        ),
+                        lhsT=ident_bf[:],
+                        rhs=raw[:, :, c0 : c0 + P].rearrange("p t c -> p c t"),
+                        start=True,
+                        stop=True,
+                    )
+                nc.scalar.copy(
+                    out=flat[:, half * 2 * BLOCK : (half + 1) * 2 * BLOCK].bitcast(F32),
+                    in_=mixed[:].bitcast(F32),
+                )
+            grouped_tiles[(b, g)] = grouped
+
+        def passes_of(b, routes):
+            if b >= len(blocks):
+                return []
+            return [g for g in range(PASSES) if ROUTES[b][g] in routes]
+
         def has_norm(b):
             return 0 <= b < len(blocks) and blocks[b][2] is not None
 
         def quantise(b):
             w_codes = codes_pool.tile([P, PASSES, BLOCK], U32, align_bytes=64, name="w_codes")
             w_scales = codes_pool.tile([P, PASSES, BLOCK], U8, align_bytes=64, name="w_scales")
-            for g in range(PASSES):
+            for g in passes_of(b, "S") + passes_of(b, "T") + passes_of(b, "V"):
                 nc.vector.quantize_mx(
                     out=w_codes[:, g, :].bitcast(FP8X4),
                     scales=w_scales[:, g, :],
@@ -223,7 +262,7 @@ def tile_gqa_flashattn_pa_kernel(
         def multiply(b):
             w_codes, w_scales = codes[b]
             for i in range(TOKEN_TILES):
-                bank = psum.tile([P, BLOCK], F32, tag="bank", name="bank")
+                bank = psum_pools[b % 2].tile([P, BLOCK], F32, tag="bank", name="bank")
                 banks[(b, i)] = bank
                 for g in range(PASSES):
                     nc.tensor.matmul_mx(
@@ -236,78 +275,88 @@ def tile_gqa_flashattn_pa_kernel(
                         stop=(g == PASSES - 1),
                     )
 
-        def scalar_copies_of(b):
-            if b >= len(blocks) or b == AHEAD - 1:
-                return 0
-            return SCALAR_COPIES
+        sums_of = {}
 
-        def scalar_work(summed, fresh):
-            copies = list(range(scalar_copies_of(fresh)))
-            for g in copies[:1]:
-                regroup(nc.scalar.copy, fresh, g)
-            if has_norm(summed):
-                sums = stats_pool.tile([P, UNITS], F32, name="sums")
-                for i in range(TOKEN_TILES):
-                    for h in range(BLOCK_HEADS):
-                        unit = h * TOKEN_TILES + i
-                        nc.scalar.activation(
-                            out=unread[:, unit, :],
-                            in_=head_sums(summed, i, h),
-                            func=ACT.Identity,
-                            accum_out=sums[:, unit : unit + 1],
-                        )
-            for g in copies[1:]:
-                regroup(nc.scalar.copy, fresh, g)
-            if has_norm(summed):
-                neg_mean = stats_pool.tile([P, UNITS], F32, name="neg_mean")
-                nc.scalar.mul(out=neg_mean[:], in_=sums[:], mul=-1.0 / HEAD)
-                squares = stats_pool.tile([P, UNITS], F32, name="squares")
-                for i in range(TOKEN_TILES):
-                    for h in range(BLOCK_HEADS):
-                        unit = h * TOKEN_TILES + i
-                        nc.scalar.activation(
-                            out=unread[:, UNITS + unit, :],
-                            in_=head_sums(summed, i, h),
-                            func=ACT.Square,
-                            bias=neg_mean[:, unit : unit + 1],
-                            accum_out=squares[:, unit : unit + 1],
-                        )
-                std = stats_pool.tile([P, UNITS], F32, name="std")
-                nc.scalar.activation(
-                    out=std[:], in_=squares[:], func=ACT.Sqrt, bias=eps[:], scale=1.0 / HEAD
-                )
-                stats[summed] = (neg_mean, std)
-            if summed == len(blocks) - 1:
-                values = result_pool.tile([P, UNITS, HEAD], F32, name="result")
-                by_tile = values[:].rearrange("p (h i) j -> p h i j", i=TOKEN_TILES)
-                for i in range(TOKEN_TILES):
-                    nc.scalar.copy(
-                        out=by_tile[:, :, i, :],
-                        in_=banks[(summed, i)][:].rearrange("p (h j) -> p h j", h=BLOCK_HEADS),
-                    )
+        def sum_heads(b):
+            sums = stats_pool.tile([P, UNITS], F32, name="sums")
+            for i in range(TOKEN_TILES):
                 for h in range(BLOCK_HEADS):
-                    store_head(summed, h, values)
+                    unit = h * TOKEN_TILES + i
+                    nc.scalar.activation(
+                        out=unread[:, unit, :],
+                        in_=head_sums(b, i, h),
+                        func=ACT.Identity,
+                        accum_out=sums[:, unit : unit + 1],
+                    )
+            neg_mean = stats_pool.tile([P, UNITS], F32, name="neg_mean")
+            nc.scalar.mul(out=neg_mean[:], in_=sums[:], mul=-1.0 / HEAD)
+            neg_means[b] = neg_mean
+
+        def square_heads(b):
+            neg_mean = neg_means[b]
+            squares = stats_pool.tile([P, UNITS], F32, name="squares")
+            for i in range(TOKEN_TILES):
+                for h in range(BLOCK_HEADS):
+                    unit = h * TOKEN_TILES + i
+                    nc.scalar.activation(
+                        out=unread[:, UNITS + unit, :],
+                        in_=head_sums(b, i, h),
+                        func=ACT.Square,
+                        bias=neg_mean[:, unit : unit + 1],
+                        accum_out=squares[:, unit : unit + 1],
+                    )
+            std = stats_pool.tile([P, UNITS], F32, name="std")
+            nc.scalar.activation(
+                out=std[:], in_=squares[:], func=ACT.Sqrt, bias=eps[:], scale=1.0 / HEAD
+            )
+            stats[b] = std
+
+        def copy_values(b):
+            values = result_pool.tile([P, UNITS, HEAD], F32, name="result")
+            by_tile = values[:].rearrange("p (h i) j -> p h i j", i=TOKEN_TILES)
+            for i in range(TOKEN_TILES):
+                nc.scalar.copy(
+                    out=by_tile[:, :, i, :],
+                    in_=banks[(b, i)][:].rearrange("p (h j) -> p h j", h=BLOCK_HEADS),
+                )
+            for h in range(BLOCK_HEADS):
+                store_head(b, h, values)
+
+        def tensor_regroups(fresh, pool):
+            for g in passes_of(fresh, "T"):
+                regroup_on_tensor(pool, fresh, g)
+
+        def scalar_regroups(fresh):
+            for g in passes_of(fresh, "S"):
+                regroup(nc.scalar.copy, fresh, g)
 
         def vector_prepare(fresh):
-            for g in range(scalar_copies_of(fresh), PASSES):
+            for g in passes_of(fresh, "V"):
                 regroup(nc.vector.tensor_copy, fresh, g)
             if fresh + AHEAD < len(blocks):
                 load_block(fresh + AHEAD)
             quantise(fresh)
 
-        for b in range(AHEAD):
-            scalar_work(-1, b)
-            vector_prepare(b)
-            if b < 2:
-                multiply(b)
-        scalar_work(0, len(blocks))
+        tensor_regroups(0, psum_pools[0])
+        scalar_regroups(0)
+        vector_prepare(0)
+        tensor_regroups(1, psum_pools[1])
+        scalar_regroups(1)
+        multiply(0)
+        vector_prepare(1)
+        scalar_regroups(2)
+        multiply(1)
+        sum_heads(0)
+        square_heads(0)
+        vector_prepare(2)
 
         for b in range(len(blocks)):
-            scalar_work(b + 1, b + AHEAD)
+            fresh = b + AHEAD
+            if has_norm(b + 1):
+                sum_heads(b + 1)
+            scalar_regroups(fresh)
             if has_norm(b):
-                neg_mean, std = stats[b]
-                rstd = stats_pool.tile([P, UNITS], F32, name="rstd")
-                nc.vector.reciprocal(out=rstd[:], in_=std[:])
+                neg_mean = neg_means[b]
                 products = products_pool.tile([P, UNITS, 2, HEAD], F32, name="products")
                 for i in range(TOKEN_TILES):
                     for h in range(BLOCK_HEADS):
@@ -321,12 +370,19 @@ def tile_gqa_flashattn_pa_kernel(
                             op1=ALU.mult,
                         )
                 result = result_pool.tile([P, UNITS, HEAD], F32, name="result")
-                add_partner_halves(nc.gpsimd, result, products)
-                rotated[b] = (rstd, result)
+                add_partner_halves(TAIL_ENGINE(nc, has_norm(b + 1)), result, products)
+                rotated[b] = result
+            tensor_regroups(fresh, psum_pools[b % 2])
+            if has_norm(b + 1):
+                square_heads(b + 1)
+            elif b + 1 == len(blocks) - 1:
+                copy_values(b + 1)
             if b + 2 < len(blocks):
                 multiply(b + 2)
             if has_norm(b - 1):
-                rstd, result = rotated[b - 1]
+                result = rotated[b - 1]
+                rstd = stats_pool.tile([P, UNITS], F32, name="rstd")
+                nc.vector.reciprocal(out=rstd[:], in_=stats[b - 1][:])
                 for h in range(BLOCK_HEADS):
                     for i in range(TOKEN_TILES):
                         unit = h * TOKEN_TILES + i
@@ -339,5 +395,5 @@ def tile_gqa_flashattn_pa_kernel(
                             op1=ALU.add,
                         )
                     store_head(b - 1, h, result)
-            if b + AHEAD < len(blocks):
-                vector_prepare(b + AHEAD)
+            if fresh < len(blocks):
+                vector_prepare(fresh)

@@ -350,11 +350,38 @@ def tile_gqa_flashattn_pa_kernel(
         square_heads(0)
         vector_prepare(2)
 
+        def finish(b, rstd):
+            result = rotated[b][1]
+            for h in range(BLOCK_HEADS):
+                for i in range(TOKEN_TILES):
+                    unit = h * TOKEN_TILES + i
+                    nc.vector.scalar_tensor_tensor(
+                        out=result[:, unit, :],
+                        in0=result[:, unit, :],
+                        scalar=rstd[:, unit : unit + 1],
+                        in1=shifts[blocks[b][2]][:, i, :],
+                        op0=ALU.mult,
+                        op1=ALU.add,
+                    )
+                store_head(b, h, result)
+
+        def invert_std(b):
+            rstd = stats_pool.tile([P, UNITS], F32, name="rstd")
+            nc.vector.reciprocal(out=rstd[:], in_=stats[b][:])
+            return rstd
+
         for b in range(len(blocks)):
             fresh = b + AHEAD
             if has_norm(b + 1):
                 sum_heads(b + 1)
             scalar_regroups(fresh)
+            if has_norm(b - 1):
+                rstd = invert_std(b - 1)
+            if has_norm(b - 1) and has_norm(b):
+                products, result = rotated[b - 1]
+                last_value = products[:, UNITS - 1, 1, HEAD - 1 : HEAD]
+                nc.vector.tensor_scalar_mul(out=last_value, in0=last_value, scalar1=1.0)
+                add_partner_halves(nc.gpsimd, result, products)
             if has_norm(b):
                 neg_mean = neg_means[b]
                 products = products_pool.tile([P, UNITS, 2, HEAD], F32, name="products")
@@ -370,8 +397,9 @@ def tile_gqa_flashattn_pa_kernel(
                             op1=ALU.mult,
                         )
                 result = result_pool.tile([P, UNITS, HEAD], F32, name="result")
-                add_partner_halves(TAIL_ENGINE(nc, has_norm(b + 1)), result, products)
-                rotated[b] = result
+                rotated[b] = (products, result)
+                if not has_norm(b + 1):
+                    add_partner_halves(nc.vector, result, products)
             tensor_regroups(fresh, psum_pools[b % 2])
             if has_norm(b + 1):
                 square_heads(b + 1)
@@ -379,21 +407,9 @@ def tile_gqa_flashattn_pa_kernel(
                 copy_values(b + 1)
             if b + 2 < len(blocks):
                 multiply(b + 2)
+            for g in passes_of(fresh, "V"):
+                regroup(nc.vector.tensor_copy, fresh, g)
             if has_norm(b - 1):
-                result = rotated[b - 1]
-                rstd = stats_pool.tile([P, UNITS], F32, name="rstd")
-                nc.vector.reciprocal(out=rstd[:], in_=stats[b - 1][:])
-                for h in range(BLOCK_HEADS):
-                    for i in range(TOKEN_TILES):
-                        unit = h * TOKEN_TILES + i
-                        nc.vector.scalar_tensor_tensor(
-                            out=result[:, unit, :],
-                            in0=result[:, unit, :],
-                            scalar=rstd[:, unit : unit + 1],
-                            in1=shifts[blocks[b - 1][2]][:, i, :],
-                            op0=ALU.mult,
-                            op1=ALU.add,
-                        )
-                    store_head(b - 1, h, result)
+                finish(b - 1, rstd)
             if fresh < len(blocks):
-                vector_prepare(fresh)
+                quantise(fresh)

@@ -26,7 +26,7 @@ UNITS = BLOCK_HEADS * TOKEN_TILES
 Q_BLOCKS = 4
 EPS = 1e-6
 AHEAD = 3
-ROUTES = ("TTVV", "TSVV", "SVVV", "TTSV", "TTSV", "TTSV")
+ROUTES = ("SSVV", "SSVV", "VVVV", "SSVV", "SSVV", "SSSV")
 
 
 def TAIL_ENGINE(nc, more):

@@ -26,7 +26,7 @@ UNITS = BLOCK_HEADS * TOKEN_TILES
 Q_BLOCKS = 4
 EPS = 1e-6
 AHEAD = 3
-ROUTES = ("SSVV", "SSVV", "VVVV", "SSVV", "SSVV", "SSSV")
+ROUTES = ("SSVV", "SSVV", "VVVV", "SSGg", "SSSV", "SSSV")
 
 
 def TAIL_ENGINE(nc, more):
@@ -209,17 +209,30 @@ def tile_gqa_flashattn_pa_kernel(
         grouped_tiles = {}
         codes = {}
 
-        def regroup(engine_copy, b, g):
-            grouped = grouped_pool.tile([P, BLOCK, PACK], BF16, align_bytes=64, name="grouped")
+        def grouped_tile(b, g):
+            if (b, g) not in grouped_tiles:
+                grouped = grouped_pool.tile([P, BLOCK, PACK], BF16, align_bytes=64, name="grouped")
+                grouped_tiles[(b, g)] = grouped
+            return grouped_tiles[(b, g)]
+
+        def regroup(engine_copy, b, g, columns=slice(0, BLOCK)):
             engine_copy(
-                out=grouped[:].rearrange("p (c r) t -> p c t r", r=4),
-                in_=raw_tiles[(b, g)][:].rearrange("p t (c r) -> p c t r", r=4),
+                out=grouped_tile(b, g)[:, columns, :].rearrange("p (c r) t -> p c t r", r=4),
+                in_=raw_tiles[(b, g)][:, :, columns].rearrange("p t (c r) -> p c t r", r=4),
             )
-            grouped_tiles[(b, g)] = grouped
+
+        def regroup_on_gpsimd(b, g, columns):
+            nc.gpsimd.tensor_scalar(
+                out=grouped_tile(b, g)[:, columns, :],
+                in0=raw_tiles[(b, g)][:, :, columns].rearrange("p t n -> p n t"),
+                scalar1=1.0,
+                scalar2=0.0,
+                op0=ALU.mult,
+                op1=ALU.add,
+            )
 
         def regroup_on_tensor(pool, b, g):
-            grouped = grouped_pool.tile([P, BLOCK, PACK], BF16, align_bytes=64, name="grouped")
-            flat = grouped[:].rearrange("p n t -> p (n t)")
+            flat = grouped_tile(b, g)[:].rearrange("p n t -> p (n t)")
             raw = raw_tiles[(b, g)]
             for half in range(2):
                 mixed = pool.tile([P, 2 * BLOCK], BF16, tag="bank", name="mixed")
@@ -238,7 +251,6 @@ def tile_gqa_flashattn_pa_kernel(
                     out=flat[:, half * 2 * BLOCK : (half + 1) * 2 * BLOCK].bitcast(F32),
                     in_=mixed[:].bitcast(F32),
                 )
-            grouped_tiles[(b, g)] = grouped
 
         def passes_of(b, routes):
             if b >= len(blocks):
@@ -251,7 +263,7 @@ def tile_gqa_flashattn_pa_kernel(
         def quantise(b):
             w_codes = codes_pool.tile([P, PASSES, BLOCK], U32, align_bytes=64, name="w_codes")
             w_scales = codes_pool.tile([P, PASSES, BLOCK], U8, align_bytes=64, name="w_scales")
-            for g in passes_of(b, "S") + passes_of(b, "T") + passes_of(b, "V"):
+            for g in passes_of(b, "S") + passes_of(b, "T") + passes_of(b, "G") + passes_of(b, "gV"):
                 nc.vector.quantize_mx(
                     out=w_codes[:, g, :].bitcast(FP8X4),
                     scales=w_scales[:, g, :],
@@ -326,6 +338,26 @@ def tile_gqa_flashattn_pa_kernel(
             for g in passes_of(fresh, "T"):
                 regroup_on_tensor(pool, fresh, g)
 
+        LEFT, RIGHT = slice(0, BLOCK // 2), slice(BLOCK // 2, BLOCK)
+
+        def gpsimd_regroups(fresh):
+            jobs = [(g, half) for g in passes_of(fresh, "Gg") for half in (LEFT, RIGHT)]
+            jobs = [job for job in jobs if ROUTES[fresh][job[0]] == "G" or job[1] == LEFT]
+            if jobs:
+                g = jobs[0][0]
+                nc.vector.tensor_copy(
+                    out=grouped_tile(fresh, g)[:, 0:1, 0:1], in_=raw_tiles[(fresh, g)][:, 0:1, 0:1]
+                )
+            for g, half in jobs:
+                regroup_on_gpsimd(fresh, g, half)
+
+        def vector_regroups(fresh):
+            for g in passes_of(fresh, "gV"):
+                if ROUTES[fresh][g] == "g":
+                    regroup(nc.vector.tensor_copy, fresh, g, RIGHT)
+                else:
+                    regroup(nc.vector.tensor_copy, fresh, g)
+
         def scalar_regroups(fresh):
             for g in passes_of(fresh, "S"):
                 regroup(nc.scalar.copy, fresh, g)
@@ -372,9 +404,9 @@ def tile_gqa_flashattn_pa_kernel(
 
         for b in range(len(blocks)):
             fresh = b + AHEAD
+            scalar_regroups(fresh)
             if has_norm(b + 1):
                 sum_heads(b + 1)
-            scalar_regroups(fresh)
             if has_norm(b - 1):
                 rstd = invert_std(b - 1)
             if has_norm(b - 1) and has_norm(b):
@@ -382,6 +414,7 @@ def tile_gqa_flashattn_pa_kernel(
                 last_value = products[:, UNITS - 1, 1, HEAD - 1 : HEAD]
                 nc.vector.tensor_scalar_mul(out=last_value, in0=last_value, scalar1=1.0)
                 add_partner_halves(nc.gpsimd, result, products)
+            gpsimd_regroups(fresh)
             if has_norm(b):
                 neg_mean = neg_means[b]
                 products = products_pool.tile([P, UNITS, 2, HEAD], F32, name="products")
@@ -407,8 +440,7 @@ def tile_gqa_flashattn_pa_kernel(
                 copy_values(b + 1)
             if b + 2 < len(blocks):
                 multiply(b + 2)
-            for g in passes_of(fresh, "V"):
-                regroup(nc.vector.tensor_copy, fresh, g)
+            vector_regroups(fresh)
             if has_norm(b - 1):
                 finish(b - 1, rstd)
             if fresh < len(blocks):

@@ -26,7 +26,7 @@ UNITS = BLOCK_HEADS * TOKEN_TILES
 Q_BLOCKS = 4
 EPS = 1e-6
 AHEAD = 3
-ROUTES = ("SSVV", "SSVV", "VVVV", "SSGg", "SSSV", "SSSV")
+ROUTES = ("SSVV", "SSVV", "VVVV", "SSGg", "SSVV", "SSSV")
 
 
 def TAIL_ENGINE(nc, more):
@@ -84,6 +84,8 @@ def tile_gqa_flashattn_pa_kernel(
                 ),
             )
 
+        vector_rows = const.tile([P, 4 * HEAD], BF16)
+        nc.vector.memset(vector_rows[:], 0.0)
         eps = const.tile([P, 1], F32)
         nc.vector.memset(eps[:], EPS)
         warm = const.tile([P, 1], F32)
@@ -95,8 +97,6 @@ def tile_gqa_flashattn_pa_kernel(
         make_identity(nc, ident_bf[:])
         ones = const.tile([P, P], BF16)
         nc.vector.memset(ones[:], 1.0)
-        vector_rows = const.tile([P, 4 * HEAD], BF16)
-        nc.vector.memset(vector_rows[:], 0.0)
         for v, vec in enumerate((q_gamma, q_beta, k_gamma, k_beta)):
             nc.sync.dma_start(
                 out=vector_rows[0:1, v * HEAD : (v + 1) * HEAD], in_=vec.unsqueeze(0)
@@ -156,11 +156,15 @@ def tile_gqa_flashattn_pa_kernel(
                         op1=ALU.mult,
                     )
 
+            beta_products = {}
             for kind, v in (("k", 2), ("q", 0)):
                 rotation_products(factors[kind], v)
-                beta_products = stage.tile([P, TOKEN_TILES, 2, HEAD], F32, name="beta_" + kind)
-                rotation_products(beta_products, v + 1)
-                add_partner_halves(nc.vector, shifts[kind], beta_products)
+                beta_products[kind] = stage.tile(
+                    [P, TOKEN_TILES, 2, HEAD], F32, name="beta_" + kind
+                )
+                rotation_products(beta_products[kind], v + 1)
+            for kind in ("k", "q"):
+                add_partner_halves(nc.vector, shifts[kind], beta_products[kind])
 
             x_words = x_sb[:].bitcast(F32).rearrange(
                 "p (i g m u) -> p i g u m", i=TOKEN_TILES, g=PASSES, u=2
@@ -263,7 +267,12 @@ def tile_gqa_flashattn_pa_kernel(
         def quantise(b):
             w_codes = codes_pool.tile([P, PASSES, BLOCK], U32, align_bytes=64, name="w_codes")
             w_scales = codes_pool.tile([P, PASSES, BLOCK], U8, align_bytes=64, name="w_scales")
-            for g in passes_of(b, "S") + passes_of(b, "T") + passes_of(b, "G") + passes_of(b, "gV"):
+            others = passes_of(b, "ST")
+            own = passes_of(b, "sV")
+            order = []
+            for n in range(PASSES):
+                order.extend(others[n : n + 1] + own[n : n + 1])
+            for g in order + passes_of(b, "Gg"):
                 nc.vector.quantize_mx(
                     out=w_codes[:, g, :].bitcast(FP8X4),
                     scales=w_scales[:, g, :],
@@ -288,6 +297,7 @@ def tile_gqa_flashattn_pa_kernel(
                     )
 
         sums_of = {}
+        squares_of = {}
 
         def sum_heads(b):
             sums = stats_pool.tile([P, UNITS], F32, name="sums")
@@ -300,8 +310,11 @@ def tile_gqa_flashattn_pa_kernel(
                         func=ACT.Identity,
                         accum_out=sums[:, unit : unit + 1],
                     )
+            sums_of[b] = sums
+
+        def negate_mean(b):
             neg_mean = stats_pool.tile([P, UNITS], F32, name="neg_mean")
-            nc.scalar.mul(out=neg_mean[:], in_=sums[:], mul=-1.0 / HEAD)
+            nc.scalar.mul(out=neg_mean[:], in_=sums_of[b][:], mul=-1.0 / HEAD)
             neg_means[b] = neg_mean
 
         def square_heads(b):
@@ -317,9 +330,12 @@ def tile_gqa_flashattn_pa_kernel(
                         bias=neg_mean[:, unit : unit + 1],
                         accum_out=squares[:, unit : unit + 1],
                     )
+            squares_of[b] = squares
+
+        def root(b):
             std = stats_pool.tile([P, UNITS], F32, name="std")
             nc.scalar.activation(
-                out=std[:], in_=squares[:], func=ACT.Sqrt, bias=eps[:], scale=1.0 / HEAD
+                out=std[:], in_=squares_of[b][:], func=ACT.Sqrt, bias=eps[:], scale=1.0 / HEAD
             )
             stats[b] = std
 
@@ -352,19 +368,21 @@ def tile_gqa_flashattn_pa_kernel(
                 regroup_on_gpsimd(fresh, g, half)
 
         def vector_regroups(fresh):
-            for g in passes_of(fresh, "gV"):
-                if ROUTES[fresh][g] == "g":
+            for g in passes_of(fresh, "sgV"):
+                if ROUTES[fresh][g] in "sg":
                     regroup(nc.vector.tensor_copy, fresh, g, RIGHT)
                 else:
                     regroup(nc.vector.tensor_copy, fresh, g)
 
+        def scalar_jobs(fresh):
+            return [(fresh, g, LEFT if ROUTES[fresh][g] == "s" else slice(0, BLOCK)) for g in passes_of(fresh, "Ss")]
+
         def scalar_regroups(fresh):
-            for g in passes_of(fresh, "S"):
-                regroup(nc.scalar.copy, fresh, g)
+            for job in scalar_jobs(fresh):
+                regroup(nc.scalar.copy, *job)
 
         def vector_prepare(fresh):
-            for g in passes_of(fresh, "V"):
-                regroup(nc.vector.tensor_copy, fresh, g)
+            vector_regroups(fresh)
             if fresh + AHEAD < len(blocks):
                 load_block(fresh + AHEAD)
             quantise(fresh)
@@ -379,6 +397,7 @@ def tile_gqa_flashattn_pa_kernel(
         scalar_regroups(2)
         multiply(1)
         sum_heads(0)
+        negate_mean(0)
         square_heads(0)
         vector_prepare(2)
 
@@ -404,11 +423,21 @@ def tile_gqa_flashattn_pa_kernel(
 
         for b in range(len(blocks)):
             fresh = b + AHEAD
-            scalar_regroups(fresh)
+            jobs = scalar_jobs(fresh)
+            for job in jobs[:-2]:
+                regroup(nc.scalar.copy, *job)
             if has_norm(b + 1):
                 sum_heads(b + 1)
+            if has_norm(b):
+                root(b)
+            for job in jobs[-2:-1]:
+                regroup(nc.scalar.copy, *job)
+            if has_norm(b + 1):
+                negate_mean(b + 1)
+            for job in jobs[-1:]:
+                regroup(nc.scalar.copy, *job)
             if has_norm(b - 1):
-                rstd = invert_std(b - 1)
+                rstd = invert_std(b - 1) if has_norm(b) else last_rstd
             if has_norm(b - 1) and has_norm(b):
                 products, result = rotated[b - 1]
                 last_value = products[:, UNITS - 1, 1, HEAD - 1 : HEAD]
@@ -438,10 +467,15 @@ def tile_gqa_flashattn_pa_kernel(
                 square_heads(b + 1)
             elif b + 1 == len(blocks) - 1:
                 copy_values(b + 1)
+            last = len(blocks) - 1
+            if b + 2 == last:
+                quantise(last)
             if b + 2 < len(blocks):
                 multiply(b + 2)
             vector_regroups(fresh)
+            if has_norm(b) and not has_norm(b + 1):
+                last_rstd = invert_std(b)
             if has_norm(b - 1):
                 finish(b - 1, rstd)
-            if fresh < len(blocks):
+            if fresh < last:
                 quantise(fresh)

@@ -37,13 +37,13 @@ FLOPS = 2 * TOKENS * D_MODEL * (Q_BLOCKS + 2) * BLOCK
 
 
 def add_partner_halves(engine, out, products):
-    for lo, partner in ((0, HALF), (HALF, 0)):
-        engine.tensor_tensor(
-            out=out[:, :, lo : lo + HALF],
-            in0=products[:, :, 0, lo : lo + HALF],
-            in1=products[:, :, 1, partner : partner + HALF],
-            op=ALU.add,
-        )
+    halves = "p n (s e) -> p n s e"
+    engine.tensor_tensor(
+        out=out[:, :, :].rearrange(halves, s=2),
+        in0=products[:, :, 0, :].rearrange(halves, s=2),
+        in1=products[:, :, 1, :].rearrange(halves, s=2)[:, :, ::-1, :],
+        op=ALU.add,
+    )
 
 
 def tile_gqa_flashattn_pa_kernel(

@@ -26,7 +26,7 @@ UNITS = BLOCK_HEADS * TOKEN_TILES
 Q_BLOCKS = 4
 EPS = 1e-6
 AHEAD = 3
-ROUTES = ("SSVV", "SSVV", "VVVV", "SSGg", "SSVV", "SSSV")
+ROUTES = ("VSSV", "SSVV", "VVVV", "SSGg", "TSsV", "TSSV")
 
 
 def TAIL_ENGINE(nc, more):
@@ -123,6 +123,21 @@ def tile_gqa_flashattn_pa_kernel(
         x_codes = const.tile([P, TOKEN_TILES, PASSES * P], U32, align_bytes=64)
         x_scales = const.tile([P, TOKEN_TILES, PASSES * P], U8, align_bytes=64)
 
+        grouped_tiles = {}
+        early = set()
+
+        def grouped_tile(b, g):
+            if (b, g) not in grouped_tiles:
+                grouped = grouped_pool.tile([P, BLOCK, PACK], BF16, align_bytes=64, name="grouped")
+                grouped_tiles[(b, g)] = grouped
+            return grouped_tiles[(b, g)]
+
+        def regroup(engine_copy, b, g, columns=slice(0, BLOCK)):
+            engine_copy(
+                out=grouped_tile(b, g)[:, columns, :].rearrange("p (c r) t -> p c t r", r=4),
+                in_=raw_tiles[(b, g)][:, :, columns].rearrange("p t (c r) -> p c t r", r=4),
+            )
+
         with tc.tile_pool(name="stage", bufs=1) as stage:
             x_sb = stage.tile([P, TOKEN_TILES * D_MODEL], BF16)
             x_rows = x.rearrange("o (p i) k -> p (o i) k", i=TOKEN_TILES)
@@ -156,15 +171,12 @@ def tile_gqa_flashattn_pa_kernel(
                         op1=ALU.mult,
                     )
 
-            beta_products = {}
+            for kind, v in (("k", 2), ("q", 0)):
+                beta_products = stage.tile([P, TOKEN_TILES, 2, HEAD], F32, name="beta_" + kind)
+                rotation_products(beta_products, v + 1)
+                add_partner_halves(nc.gpsimd, shifts[kind], beta_products)
             for kind, v in (("k", 2), ("q", 0)):
                 rotation_products(factors[kind], v)
-                beta_products[kind] = stage.tile(
-                    [P, TOKEN_TILES, 2, HEAD], F32, name="beta_" + kind
-                )
-                rotation_products(beta_products[kind], v + 1)
-            for kind in ("k", "q"):
-                add_partner_halves(nc.vector, shifts[kind], beta_products[kind])
 
             x_words = x_sb[:].bitcast(F32).rearrange(
                 "p (i g m u) -> p i g u m", i=TOKEN_TILES, g=PASSES, u=2
@@ -197,6 +209,9 @@ def tile_gqa_flashattn_pa_kernel(
                     scales=x_scales[:, i, :],
                     in_=x_grouped[i][:],
                 )
+                if i == 1:
+                    regroup(nc.vector.tensor_copy, 0, ROUTES[0].index("V"))
+                    early.add((0, ROUTES[0].index("V")))
 
         late = ctx.enter_context(tc.tile_pool(name="late", bufs=1))
         products_pool = ctx.enter_context(tc.tile_pool(name="products", bufs=2))
@@ -210,20 +225,7 @@ def tile_gqa_flashattn_pa_kernel(
         def head_sums(b, i, h):
             return banks[(b, i)][:, h * HEAD : (h + 1) * HEAD]
 
-        grouped_tiles = {}
         codes = {}
-
-        def grouped_tile(b, g):
-            if (b, g) not in grouped_tiles:
-                grouped = grouped_pool.tile([P, BLOCK, PACK], BF16, align_bytes=64, name="grouped")
-                grouped_tiles[(b, g)] = grouped
-            return grouped_tiles[(b, g)]
-
-        def regroup(engine_copy, b, g, columns=slice(0, BLOCK)):
-            engine_copy(
-                out=grouped_tile(b, g)[:, columns, :].rearrange("p (c r) t -> p c t r", r=4),
-                in_=raw_tiles[(b, g)][:, :, columns].rearrange("p t (c r) -> p c t r", r=4),
-            )
 
         def regroup_on_gpsimd(b, g, columns):
             nc.gpsimd.tensor_scalar(
@@ -369,6 +371,8 @@ def tile_gqa_flashattn_pa_kernel(
 
         def vector_regroups(fresh):
             for g in passes_of(fresh, "sgV"):
+                if (fresh, g) in early:
+                    continue
                 if ROUTES[fresh][g] in "sg":
                     regroup(nc.vector.tensor_copy, fresh, g, RIGHT)
                 else:

@@ -25,13 +25,9 @@ BLOCK = BLOCK_HEADS * HEAD
 UNITS = BLOCK_HEADS * TOKEN_TILES
 Q_BLOCKS = 4
 EPS = 1e-6
-AHEAD = 3
-ROUTES = ("VSSV", "SSVV", "VVVV", "SSGg", "TSsV", "TSSV")
-
-
-def TAIL_ENGINE(nc, more):
-    return nc.gpsimd if more else nc.vector
-
+AHEAD = 2
+RAW_TILES = 16
+RING = 7
 
 FLOPS = 2 * TOKENS * D_MODEL * (Q_BLOCKS + 2) * BLOCK
 
@@ -53,19 +49,24 @@ def tile_gqa_flashattn_pa_kernel(
     with ExitStack() as ctx:
         ctx.enter_context(tc.manual_schedule())
         const = ctx.enter_context(tc.tile_pool(name="const", bufs=1))
-        raw_pool = ctx.enter_context(tc.tile_pool(name="raw", bufs=AHEAD * PASSES))
+        raw_pool = ctx.enter_context(tc.tile_pool(name="raw", bufs=RAW_TILES))
         grouped_pool = ctx.enter_context(tc.tile_pool(name="grouped", bufs=2 * PASSES))
-        codes_pool = ctx.enter_context(tc.tile_pool(name="codes", bufs=AHEAD))
+        codes_pool = ctx.enter_context(tc.tile_pool(name="codes", bufs=3))
         stats_pool = ctx.enter_context(tc.tile_pool(name="stats", bufs=4))
-        psum_pools = (
-            ctx.enter_context(tc.psum_pool(name="psum_even", bufs=TOKEN_TILES)),
-            ctx.enter_context(tc.psum_pool(name="psum_odd", bufs=TOKEN_TILES)),
-        )
+        psum = ctx.enter_context(tc.psum_pool(name="psum", bufs=1))
+
+        def bank_tile(n, name, width=P * PACK, dtype=F32):
+            return psum.tile([P, width], dtype, tag="bank%d" % n, name=name)
+
+        def bank_of(b, i):
+            if b < 2:
+                return TOKEN_TILES * b + i
+            return (TOKEN_TILES * (b - 2) + i) % RING
 
         def heads_of(out):
             return out.rearrange("o h (p i) j -> p (o h) (i j)", i=TOKEN_TILES)
 
-        blocks = [(Wk, heads_of(k_rot), "k")]
+        blocks = []
         for c in range(Q_BLOCKS):
             blocks.append(
                 (
@@ -74,6 +75,7 @@ def tile_gqa_flashattn_pa_kernel(
                     "q",
                 )
             )
+        blocks.append((Wk, heads_of(k_rot), "k"))
         blocks.append((Wv, heads_of(v_out), None))
 
         def store_head(b, h, result):
@@ -89,7 +91,7 @@ def tile_gqa_flashattn_pa_kernel(
         eps = const.tile([P, 1], F32)
         nc.vector.memset(eps[:], EPS)
         warm = const.tile([P, 1], F32)
-        nc.scalar.sqrt(out=warm[:], in_=eps[:])
+        nc.scalar.activation(out=warm[:], in_=eps[:], func=ACT.Abs_reciprocal_sqrt)
 
         ident = const.tile([P, P], F32)
         make_identity(nc, ident[:])
@@ -120,6 +122,7 @@ def tile_gqa_flashattn_pa_kernel(
         for kind in ("k", "q"):
             factors[kind] = const.tile([P, TOKEN_TILES, 2, HEAD], F32, name="factors_" + kind)
             shifts[kind] = const.tile([P, TOKEN_TILES, HEAD], F32, name="shift_" + kind)
+        LEFT, RIGHT = slice(0, BLOCK // 2), slice(BLOCK // 2, BLOCK)
         x_codes = const.tile([P, TOKEN_TILES, PASSES * P], U32, align_bytes=64)
         x_scales = const.tile([P, TOKEN_TILES, PASSES * P], U8, align_bytes=64)
 
@@ -145,10 +148,10 @@ def tile_gqa_flashattn_pa_kernel(
                 nc.sync.dma_start(
                     out=x_sb[:, i * D_MODEL : (i + 1) * D_MODEL], in_=x_rows[:, i, :]
                 )
-            for b in range(AHEAD):
+            for b in range(RAW_TILES // PASSES):
                 load_block(b)
 
-            spread_ps = psum_pools[0].tile([P, 4 * HEAD], F32, tag="bank", name="spread_ps")
+            spread_ps = bank_tile(0, "spread_ps")
             nc.tensor.matmul(
                 out=spread_ps[:], lhsT=ones[:], rhs=vector_rows[:], start=True, stop=True
             )
@@ -171,11 +174,11 @@ def tile_gqa_flashattn_pa_kernel(
                         op1=ALU.mult,
                     )
 
-            for kind, v in (("k", 2), ("q", 0)):
+            for kind, v in (("q", 0), ("k", 2)):
                 beta_products = stage.tile([P, TOKEN_TILES, 2, HEAD], F32, name="beta_" + kind)
                 rotation_products(beta_products, v + 1)
                 add_partner_halves(nc.gpsimd, shifts[kind], beta_products)
-            for kind, v in (("k", 2), ("q", 0)):
+            for kind, v in (("q", 0), ("k", 2)):
                 rotation_products(factors[kind], v)
 
             x_words = x_sb[:].bitcast(F32).rearrange(
@@ -191,7 +194,7 @@ def tile_gqa_flashattn_pa_kernel(
                     "p (g s u) -> p g s u", g=PASSES, u=2
                 )
                 for pair in range(PASSES // 2):
-                    xt = psum_pools[1].tile([P, 4 * P], F32, tag="bank", name="xt")
+                    xt = bank_tile(RING - 4 + (2 * i + pair) % 4, "xt")
                     for g2 in range(2):
                         for u in range(2):
                             nc.tensor.transpose(
@@ -210,13 +213,15 @@ def tile_gqa_flashattn_pa_kernel(
                     in_=x_grouped[i][:],
                 )
                 if i == 1:
-                    regroup(nc.vector.tensor_copy, 0, ROUTES[0].index("V"))
-                    early.add((0, ROUTES[0].index("V")))
+                    regroup(nc.vector.tensor_copy, 0, 0)
+                    early.add((0, 0))
 
         late = ctx.enter_context(tc.tile_pool(name="late", bufs=1))
         products_pool = ctx.enter_context(tc.tile_pool(name="products", bufs=2))
         result_pool = ctx.enter_context(tc.tile_pool(name="result", bufs=3))
-        unread = late.tile([P, 2 * UNITS, HEAD], BF16)
+        unread = late.tile([P, UNITS, HEAD], BF16)
+        copies_pool = ctx.enter_context(tc.tile_pool(name="copies", bufs=2))
+        copies = {}
         banks = {}
         neg_means = {}
         stats = {}
@@ -237,19 +242,19 @@ def tile_gqa_flashattn_pa_kernel(
                 op1=ALU.add,
             )
 
-        def regroup_on_tensor(pool, b, g):
+        def regroup_on_tensor(b, g, bank_numbers):
             flat = grouped_tile(b, g)[:].rearrange("p n t -> p (n t)")
             raw = raw_tiles[(b, g)]
             for half in range(2):
-                mixed = pool.tile([P, 2 * BLOCK], BF16, tag="bank", name="mixed")
+                mixed = bank_tile(bank_numbers[half], "mixed", 2 * BLOCK, BF16)
                 for q in range(2):
                     c0 = (2 * half + q) * P
                     nc.tensor.matmul(
                         out=mixed[:, q * BLOCK : (q + 1) * BLOCK].rearrange(
-                            "p (c t) -> p c t", t=PACK
+                            "p (c t) -> p t c", t=PACK
                         ),
                         lhsT=ident_bf[:],
-                        rhs=raw[:, :, c0 : c0 + P].rearrange("p t c -> p c t"),
+                        rhs=raw[:, :, c0 : c0 + P],
                         start=True,
                         stop=True,
                     )
@@ -258,34 +263,10 @@ def tile_gqa_flashattn_pa_kernel(
                     in_=mixed[:].bitcast(F32),
                 )
 
-        def passes_of(b, routes):
-            if b >= len(blocks):
-                return []
-            return [g for g in range(PASSES) if ROUTES[b][g] in routes]
-
-        def has_norm(b):
-            return 0 <= b < len(blocks) and blocks[b][2] is not None
-
-        def quantise(b):
-            w_codes = codes_pool.tile([P, PASSES, BLOCK], U32, align_bytes=64, name="w_codes")
-            w_scales = codes_pool.tile([P, PASSES, BLOCK], U8, align_bytes=64, name="w_scales")
-            others = passes_of(b, "ST")
-            own = passes_of(b, "sV")
-            order = []
-            for n in range(PASSES):
-                order.extend(others[n : n + 1] + own[n : n + 1])
-            for g in order + passes_of(b, "Gg"):
-                nc.vector.quantize_mx(
-                    out=w_codes[:, g, :].bitcast(FP8X4),
-                    scales=w_scales[:, g, :],
-                    in_=grouped_tiles[(b, g)][:].rearrange("p n t -> p (n t)"),
-                )
-            codes[b] = (w_codes, w_scales)
-
-        def multiply(b):
+        def multiply(b, tiles):
             w_codes, w_scales = codes[b]
-            for i in range(TOKEN_TILES):
-                bank = psum_pools[b % 2].tile([P, BLOCK], F32, tag="bank", name="bank")
+            for i in tiles:
+                bank = bank_tile(bank_of(b, i), "bank")
                 banks[(b, i)] = bank
                 for g in range(PASSES):
                     nc.tensor.matmul_mx(
@@ -303,11 +284,12 @@ def tile_gqa_flashattn_pa_kernel(
 
         def sum_heads(b):
             sums = stats_pool.tile([P, UNITS], F32, name="sums")
+            copies[b] = copies_pool.tile([P, UNITS, HEAD], F32, name="copies")
             for i in range(TOKEN_TILES):
                 for h in range(BLOCK_HEADS):
                     unit = h * TOKEN_TILES + i
                     nc.scalar.activation(
-                        out=unread[:, unit, :],
+                        out=copies[b][:, unit, :],
                         in_=head_sums(b, i, h),
                         func=ACT.Identity,
                         accum_out=sums[:, unit : unit + 1],
@@ -326,20 +308,24 @@ def tile_gqa_flashattn_pa_kernel(
                 for h in range(BLOCK_HEADS):
                     unit = h * TOKEN_TILES + i
                     nc.scalar.activation(
-                        out=unread[:, UNITS + unit, :],
-                        in_=head_sums(b, i, h),
+                        out=unread[:, unit, :],
+                        in_=copies[b][:, unit, :],
                         func=ACT.Square,
                         bias=neg_mean[:, unit : unit + 1],
                         accum_out=squares[:, unit : unit + 1],
                     )
             squares_of[b] = squares
 
-        def root(b):
-            std = stats_pool.tile([P, UNITS], F32, name="std")
+        def invert_std(b):
+            rstd = stats_pool.tile([P, UNITS], F32, name="rstd")
             nc.scalar.activation(
-                out=std[:], in_=squares_of[b][:], func=ACT.Sqrt, bias=eps[:], scale=1.0 / HEAD
+                out=rstd[:],
+                in_=squares_of[b][:],
+                func=ACT.Abs_reciprocal_sqrt,
+                bias=eps[:],
+                scale=1.0 / HEAD,
             )
-            stats[b] = std
+            rstds[b] = rstd
 
         def copy_values(b):
             values = result_pool.tile([P, UNITS, HEAD], F32, name="result")
@@ -352,60 +338,13 @@ def tile_gqa_flashattn_pa_kernel(
             for h in range(BLOCK_HEADS):
                 store_head(b, h, values)
 
-        def tensor_regroups(fresh, pool):
-            for g in passes_of(fresh, "T"):
-                regroup_on_tensor(pool, fresh, g)
-
         LEFT, RIGHT = slice(0, BLOCK // 2), slice(BLOCK // 2, BLOCK)
 
-        def gpsimd_regroups(fresh):
-            jobs = [(g, half) for g in passes_of(fresh, "Gg") for half in (LEFT, RIGHT)]
-            jobs = [job for job in jobs if ROUTES[fresh][job[0]] == "G" or job[1] == LEFT]
-            if jobs:
-                g = jobs[0][0]
-                nc.vector.tensor_copy(
-                    out=grouped_tile(fresh, g)[:, 0:1, 0:1], in_=raw_tiles[(fresh, g)][:, 0:1, 0:1]
-                )
-            for g, half in jobs:
-                regroup_on_gpsimd(fresh, g, half)
+        def load_next(b):
+            if b + RAW_TILES // PASSES < len(blocks):
+                load_block(b + RAW_TILES // PASSES)
 
-        def vector_regroups(fresh):
-            for g in passes_of(fresh, "sgV"):
-                if (fresh, g) in early:
-                    continue
-                if ROUTES[fresh][g] in "sg":
-                    regroup(nc.vector.tensor_copy, fresh, g, RIGHT)
-                else:
-                    regroup(nc.vector.tensor_copy, fresh, g)
-
-        def scalar_jobs(fresh):
-            return [(fresh, g, LEFT if ROUTES[fresh][g] == "s" else slice(0, BLOCK)) for g in passes_of(fresh, "Ss")]
-
-        def scalar_regroups(fresh):
-            for job in scalar_jobs(fresh):
-                regroup(nc.scalar.copy, *job)
-
-        def vector_prepare(fresh):
-            vector_regroups(fresh)
-            if fresh + AHEAD < len(blocks):
-                load_block(fresh + AHEAD)
-            quantise(fresh)
-
-        tensor_regroups(0, psum_pools[0])
-        scalar_regroups(0)
-        vector_prepare(0)
-        tensor_regroups(1, psum_pools[1])
-        scalar_regroups(1)
-        multiply(0)
-        vector_prepare(1)
-        scalar_regroups(2)
-        multiply(1)
-        sum_heads(0)
-        negate_mean(0)
-        square_heads(0)
-        vector_prepare(2)
-
-        def finish(b, rstd):
+        def finish(b):
             result = rotated[b][1]
             for h in range(BLOCK_HEADS):
                 for i in range(TOKEN_TILES):
@@ -413,73 +352,165 @@ def tile_gqa_flashattn_pa_kernel(
                     nc.vector.scalar_tensor_tensor(
                         out=result[:, unit, :],
                         in0=result[:, unit, :],
-                        scalar=rstd[:, unit : unit + 1],
+                        scalar=rstds[b][:, unit : unit + 1],
                         in1=shifts[blocks[b][2]][:, i, :],
                         op0=ALU.mult,
                         op1=ALU.add,
                     )
                 store_head(b, h, result)
 
-        def invert_std(b):
-            rstd = stats_pool.tile([P, UNITS], F32, name="rstd")
-            nc.vector.reciprocal(out=rstd[:], in_=stats[b][:])
-            return rstd
+        rstds = {}
 
-        for b in range(len(blocks)):
-            fresh = b + AHEAD
-            jobs = scalar_jobs(fresh)
-            for job in jobs[:-2]:
-                regroup(nc.scalar.copy, *job)
-            if has_norm(b + 1):
-                sum_heads(b + 1)
-            if has_norm(b):
-                root(b)
-            for job in jobs[-2:-1]:
-                regroup(nc.scalar.copy, *job)
-            if has_norm(b + 1):
-                negate_mean(b + 1)
-            for job in jobs[-1:]:
-                regroup(nc.scalar.copy, *job)
-            if has_norm(b - 1):
-                rstd = invert_std(b - 1) if has_norm(b) else last_rstd
-            if has_norm(b - 1) and has_norm(b):
-                products, result = rotated[b - 1]
-                last_value = products[:, UNITS - 1, 1, HEAD - 1 : HEAD]
-                nc.vector.tensor_scalar_mul(out=last_value, in0=last_value, scalar1=1.0)
-                add_partner_halves(nc.gpsimd, result, products)
-            gpsimd_regroups(fresh)
-            if has_norm(b):
-                neg_mean = neg_means[b]
-                products = products_pool.tile([P, UNITS, 2, HEAD], F32, name="products")
-                for i in range(TOKEN_TILES):
-                    for h in range(BLOCK_HEADS):
-                        unit = h * TOKEN_TILES + i
-                        nc.vector.scalar_tensor_tensor(
-                            out=products[:, unit, :, :],
-                            in0=head_sums(b, i, h).unsqueeze(1).to_broadcast([P, 2, HEAD]),
-                            scalar=neg_mean[:, unit : unit + 1],
-                            in1=factors[blocks[b][2]][:, i, :, :],
-                            op0=ALU.add,
-                            op1=ALU.mult,
-                        )
-                result = result_pool.tile([P, UNITS, HEAD], F32, name="result")
-                rotated[b] = (products, result)
-                if not has_norm(b + 1):
-                    add_partner_halves(nc.vector, result, products)
-            tensor_regroups(fresh, psum_pools[b % 2])
-            if has_norm(b + 1):
-                square_heads(b + 1)
-            elif b + 1 == len(blocks) - 1:
-                copy_values(b + 1)
-            last = len(blocks) - 1
-            if b + 2 == last:
-                quantise(last)
-            if b + 2 < len(blocks):
-                multiply(b + 2)
-            vector_regroups(fresh)
-            if has_norm(b) and not has_norm(b + 1):
-                last_rstd = invert_std(b)
-            if has_norm(b - 1):
-                finish(b - 1, rstd)
-            if fresh < last:
-                quantise(fresh)
+        HALVES = (slice(0, UNITS // 2), slice(UNITS // 2, UNITS))
+
+        def add_units(engine, b, units):
+            products, result = rotated[b]
+            add_partner_halves(engine, result[:, units, :], products[:, units, :, :])
+
+        last = len(blocks) - 1
+        FULL = slice(0, BLOCK)
+
+        def tick(b):
+            values = rotated[b][0][:, UNITS // 2 - 1 :: UNITS // 2, 1, HEAD - 1 : HEAD]
+            nc.vector.tensor_scalar_mul(out=values, in0=values, scalar1=1.0)
+            for units in HALVES:
+                add_units(nc.gpsimd, b, units)
+
+        def shift_to_psum():
+            shift_ps = bank_tile(RING, "shift_ps")
+            nc.tensor.matmul(
+                out=shift_ps[:],
+                lhsT=ident[:],
+                rhs=shifts["q"][:].rearrange("p i j -> p (i j)"),
+                start=True,
+                stop=True,
+            )
+            shifts["q"] = shift_ps[:].rearrange("p (i j) -> p i j", i=TOKEN_TILES)
+
+        def products_of(b, tiles):
+            if b not in rotated:
+                rotated[b] = (
+                    products_pool.tile([P, UNITS, 2, HEAD], F32, name="products"),
+                    result_pool.tile([P, UNITS, HEAD], F32, name="result"),
+                )
+            products, result = rotated[b]
+            neg_mean = neg_means[b]
+            for i in tiles:
+                for h in range(BLOCK_HEADS):
+                    unit = h * TOKEN_TILES + i
+                    nc.vector.scalar_tensor_tensor(
+                        out=products[:, unit, :, :],
+                        in0=head_sums(b, i, h).unsqueeze(1).to_broadcast([P, 2, HEAD]),
+                        scalar=neg_mean[:, unit : unit + 1],
+                        in1=factors[blocks[b][2]][:, i, :, :],
+                        op0=ALU.add,
+                        op1=ALU.mult,
+                    )
+
+        def quantise_passes(b, gs):
+            if b not in codes:
+                w_codes = codes_pool.tile([P, PASSES, BLOCK], U32, align_bytes=64, name="w_codes")
+                w_scales = codes_pool.tile([P, PASSES, BLOCK], U8, align_bytes=64, name="w_scales")
+                codes[b] = (w_codes, w_scales)
+            w_codes, w_scales = codes[b]
+            for g in gs:
+                nc.vector.quantize_mx(
+                    out=w_codes[:, g, :].bitcast(FP8X4),
+                    scales=w_scales[:, g, :],
+                    in_=grouped_tiles[(b, g)][:].rearrange("p n t -> p (n t)"),
+                )
+
+        def hold_gpsimd(b, g):
+            nc.vector.tensor_copy(
+                out=grouped_tile(b, g)[:, 0:1, 0:1], in_=raw_tiles[(b, g)][:, 0:1, 0:1]
+            )
+
+        regroup(nc.scalar.copy, 0, 1)
+        regroup_on_tensor(0, 2, (5, 6))
+        regroup(nc.vector.tensor_copy, 0, 3)
+        quantise_passes(0, (0, 1, 3, 2))
+        regroup(nc.scalar.copy, 1, 0)
+        multiply(0, (0, 1, 2, 3))
+        regroup(nc.vector.tensor_copy, 1, 1)
+        regroup(nc.vector.tensor_copy, 1, 2)
+        regroup(nc.vector.tensor_copy, 1, 3)
+        load_next(0)
+        quantise_passes(1, (1, 2, 3, 0))
+        sum_heads(0)
+        negate_mean(0)
+        multiply(1, (0, 1, 2, 3))
+        load_next(1)
+        regroup(nc.scalar.copy, 2, 0)
+        regroup(nc.vector.tensor_copy, 2, 1)
+        regroup(nc.vector.tensor_copy, 2, 2)
+        regroup(nc.vector.tensor_copy, 2, 3)
+        quantise_passes(2, (1, 2, 3, 0))
+        hold_gpsimd(3, 2)
+        regroup_on_gpsimd(3, 2, LEFT)
+        regroup_on_gpsimd(3, 2, RIGHT)
+        regroup_on_gpsimd(3, 3, LEFT)
+        products_of(0, (0, 1, 2, 3))
+        multiply(2, (0, 1, 2, 3))
+        sum_heads(1)
+        negate_mean(1)
+        square_heads(0)
+        invert_std(0)
+        regroup(nc.scalar.copy, 3, 0)
+        regroup(nc.scalar.copy, 3, 1)
+        tick(0)
+        regroup_on_gpsimd(3, 3, RIGHT)
+        products_of(1, (3,))
+        shift_to_psum()
+        products_of(1, (0, 1, 2))
+        sum_heads(2)
+        negate_mean(2)
+        regroup_on_tensor(4, 1, (4, 5))
+        regroup_on_tensor(4, 2, (6, 4))
+        square_heads(1)
+        invert_std(1)
+        regroup(nc.scalar.copy, 4, 0, LEFT)
+        finish(0)
+        quantise_passes(3, (0, 1, 3, 2))
+        multiply(3, (0, 1, 2))
+        tick(1)
+        regroup_on_gpsimd(4, 3, LEFT)
+        products_of(2, (0,))
+        multiply(3, (3,))
+        products_of(2, (1, 2, 3))
+        sum_heads(3)
+        negate_mean(3)
+        regroup_on_tensor(5, 1, (1, 2))
+        regroup_on_tensor(5, 2, (3, 1))
+        square_heads(2)
+        invert_std(2)
+        regroup(nc.scalar.copy, 5, 0, LEFT)
+        finish(1)
+        regroup(nc.vector.tensor_copy, 4, 0, RIGHT)
+        regroup(nc.vector.tensor_copy, 4, 3, RIGHT)
+        quantise_passes(4, (0, 1, 2, 3))
+        multiply(4, (0, 1, 2))
+        tick(2)
+        regroup_on_gpsimd(5, 3, LEFT)
+        products_of(3, (0,))
+        multiply(4, (3,))
+        products_of(3, (1, 2, 3))
+        sum_heads(4)
+        negate_mean(4)
+        square_heads(3)
+        invert_std(3)
+        finish(2)
+        regroup(nc.vector.tensor_copy, 5, 0, RIGHT)
+        regroup(nc.vector.tensor_copy, 5, 3, RIGHT)
+        quantise_passes(5, (0, 1, 2, 3))
+        multiply(5, (0, 1, 2))
+        tick(3)
+        products_of(4, (0,))
+        multiply(5, (3,))
+        products_of(4, (1, 2, 3))
+        copy_values(5)
+        square_heads(4)
+        invert_std(4)
+        add_units(nc.gpsimd, 4, HALVES[0])
+        finish(3)
+        add_units(nc.vector, 4, HALVES[1])
+        finish(4)

@@ -27,6 +27,7 @@ Q_BLOCKS = 4
 EPS = 1e-6
 AHEAD = 2
 RAW_TILES = 16
+LAST_SHARE = 6
 RING = 7
 
 FLOPS = 2 * TOKENS * D_MODEL * (Q_BLOCKS + 2) * BLOCK
@@ -50,7 +51,7 @@ def tile_gqa_flashattn_pa_kernel(
         ctx.enter_context(tc.manual_schedule())
         const = ctx.enter_context(tc.tile_pool(name="const", bufs=1))
         raw_pool = ctx.enter_context(tc.tile_pool(name="raw", bufs=RAW_TILES))
-        grouped_pool = ctx.enter_context(tc.tile_pool(name="grouped", bufs=2 * PASSES))
+        grouped_pool = ctx.enter_context(tc.tile_pool(name="grouped", bufs=1))
         codes_pool = ctx.enter_context(tc.tile_pool(name="codes", bufs=3))
         stats_pool = ctx.enter_context(tc.tile_pool(name="stats", bufs=4))
         psum = ctx.enter_context(tc.psum_pool(name="psum", bufs=1))
@@ -99,8 +100,8 @@ def tile_gqa_flashattn_pa_kernel(
         make_identity(nc, ident_bf[:])
         ones = const.tile([P, P], BF16)
         nc.vector.memset(ones[:], 1.0)
-        for v, vec in enumerate((q_gamma, q_beta, k_gamma, k_beta)):
-            nc.sync.dma_start(
+        for v, vec in ((1, q_beta), (3, k_beta), (0, q_gamma), (2, k_gamma)):
+            nc.scalar.dma_start(
                 out=vector_rows[0:1, v * HEAD : (v + 1) * HEAD], in_=vec.unsqueeze(0)
             )
         cos_sb = const.tile([P, TOKEN_TILES, HEAD], BF16)
@@ -131,7 +132,13 @@ def tile_gqa_flashattn_pa_kernel(
 
         def grouped_tile(b, g):
             if (b, g) not in grouped_tiles:
-                grouped = grouped_pool.tile([P, BLOCK, PACK], BF16, align_bytes=64, name="grouped")
+                grouped = grouped_pool.tile(
+                    [P, BLOCK, PACK],
+                    BF16,
+                    align_bytes=64,
+                    tag="grouped%d" % (PASSES * (b % 2) + g),
+                    name="grouped",
+                )
                 grouped_tiles[(b, g)] = grouped
             return grouped_tiles[(b, g)]
 
@@ -152,9 +159,15 @@ def tile_gqa_flashattn_pa_kernel(
                 load_block(b)
 
             spread_ps = bank_tile(0, "spread_ps")
-            nc.tensor.matmul(
-                out=spread_ps[:], lhsT=ones[:], rhs=vector_rows[:], start=True, stop=True
-            )
+            for v in (1, 3, 0, 2):
+                part = slice(v * HEAD, (v + 1) * HEAD)
+                nc.tensor.matmul(
+                    out=spread_ps[:, part],
+                    lhsT=ones[:],
+                    rhs=vector_rows[:, part],
+                    start=True,
+                    stop=True,
+                )
             spread = spread_ps[:].rearrange("p (v j) -> p v j", v=4)
 
             def rotation_products(out, v):
@@ -279,6 +292,7 @@ def tile_gqa_flashattn_pa_kernel(
                         stop=(g == PASSES - 1),
                     )
 
+        values_of = {}
         sums_of = {}
         squares_of = {}
 
@@ -301,10 +315,12 @@ def tile_gqa_flashattn_pa_kernel(
             nc.scalar.mul(out=neg_mean[:], in_=sums_of[b][:], mul=-1.0 / HEAD)
             neg_means[b] = neg_mean
 
-        def square_heads(b):
+        def square_heads(b, tiles=range(TOKEN_TILES)):
             neg_mean = neg_means[b]
-            squares = stats_pool.tile([P, UNITS], F32, name="squares")
-            for i in range(TOKEN_TILES):
+            if b not in squares_of:
+                squares_of[b] = stats_pool.tile([P, UNITS], F32, name="squares")
+            squares = squares_of[b]
+            for i in tiles:
                 for h in range(BLOCK_HEADS):
                     unit = h * TOKEN_TILES + i
                     nc.scalar.activation(
@@ -314,6 +330,50 @@ def tile_gqa_flashattn_pa_kernel(
                         bias=neg_mean[:, unit : unit + 1],
                         accum_out=squares[:, unit : unit + 1],
                     )
+
+        moments_of = {}
+        spreads_of = {}
+
+        def bn_heads(b, tiles=range(TOKEN_TILES)):
+            if b not in moments_of:
+                moments_of[b] = stats_pool.tile([P, UNITS, 6], F32, name="moments")
+            for i in tiles:
+                for h in range(BLOCK_HEADS):
+                    nc.vector.bn_stats(
+                        out=moments_of[b][:, h * TOKEN_TILES + i, :], in_=head_sums(b, i, h)
+                    )
+
+        def join_moments(b):
+            moments = moments_of[b]
+            total = stats_pool.tile([P, UNITS], F32, name="total")
+            nc.vector.tensor_tensor(
+                out=total[:], in0=moments[:, :, 1], in1=moments[:, :, 4], op=ALU.add
+            )
+            gap = stats_pool.tile([P, UNITS], F32, name="gap")
+            nc.vector.tensor_tensor(
+                out=gap[:], in0=moments[:, :, 1], in1=moments[:, :, 4], op=ALU.subtract
+            )
+            within = stats_pool.tile([P, UNITS], F32, name="within")
+            nc.vector.tensor_tensor(
+                out=within[:], in0=moments[:, :, 2], in1=moments[:, :, 5], op=ALU.add
+            )
+            spreads_of[b] = (total, gap, within)
+
+        def bn_mean(b):
+            total, gap, within = spreads_of[b]
+            neg_mean = stats_pool.tile([P, UNITS], F32, name="neg_mean")
+            nc.vector.tensor_scalar_mul(out=neg_mean[:], in0=total[:], scalar1=-0.5)
+            neg_means[b] = neg_mean
+            between = stats_pool.tile([P, UNITS], F32, name="between")
+            nc.vector.scalar_tensor_tensor(
+                out=between[:], in0=gap[:], scalar=HEAD / 4, in1=gap[:], op0=ALU.mult, op1=ALU.mult
+            )
+            spreads_of[b] = (between, within)
+
+        def bn_squares(b):
+            between, within = spreads_of[b]
+            squares = stats_pool.tile([P, UNITS], F32, name="squares")
+            nc.vector.tensor_tensor(out=squares[:], in0=within[:], in1=between[:], op=ALU.add)
             squares_of[b] = squares
 
         def invert_std(b):
@@ -335,8 +395,11 @@ def tile_gqa_flashattn_pa_kernel(
                     out=by_tile[:, :, i, :],
                     in_=banks[(b, i)][:].rearrange("p (h j) -> p h j", h=BLOCK_HEADS),
                 )
+            values_of[b] = values
+
+        def store_values(b):
             for h in range(BLOCK_HEADS):
-                store_head(b, h, values)
+                store_head(b, h, values_of[b])
 
         LEFT, RIGHT = slice(0, BLOCK // 2), slice(BLOCK // 2, BLOCK)
 
@@ -426,51 +489,55 @@ def tile_gqa_flashattn_pa_kernel(
             )
 
         regroup(nc.scalar.copy, 0, 1)
-        regroup_on_tensor(0, 2, (5, 6))
+        regroup(nc.scalar.copy, 0, 2)
         regroup(nc.vector.tensor_copy, 0, 3)
-        quantise_passes(0, (0, 1, 3, 2))
+        quantise_passes(0, (0, 3, 1, 2))
         regroup(nc.scalar.copy, 1, 0)
+        regroup(nc.scalar.copy, 1, 1)
         multiply(0, (0, 1, 2, 3))
-        regroup(nc.vector.tensor_copy, 1, 1)
         regroup(nc.vector.tensor_copy, 1, 2)
         regroup(nc.vector.tensor_copy, 1, 3)
         load_next(0)
-        quantise_passes(1, (1, 2, 3, 0))
-        sum_heads(0)
-        negate_mean(0)
+        quantise_passes(1, (2, 3, 0, 1))
+        regroup(nc.scalar.copy, 2, 0)
         multiply(1, (0, 1, 2, 3))
         load_next(1)
-        regroup(nc.scalar.copy, 2, 0)
-        regroup(nc.vector.tensor_copy, 2, 1)
-        regroup(nc.vector.tensor_copy, 2, 2)
+        hold_gpsimd(2, 2)
+        regroup_on_gpsimd(2, 2, LEFT)
+        bn_heads(0)
+        join_moments(0)
         regroup(nc.vector.tensor_copy, 2, 3)
-        quantise_passes(2, (1, 2, 3, 0))
+        bn_mean(0)
+        regroup(nc.vector.tensor_copy, 2, 2, RIGHT)
+        bn_squares(0)
+        regroup(nc.scalar.copy, 2, 1)
+        quantise_passes(2, (3, 0, 1, 2))
         hold_gpsimd(3, 2)
-        regroup_on_gpsimd(3, 2, LEFT)
-        regroup_on_gpsimd(3, 2, RIGHT)
-        regroup_on_gpsimd(3, 3, LEFT)
+        regroup_on_gpsimd(3, 2, slice(0, BLOCK))
+        regroup_on_gpsimd(3, 3, slice(0, 128))
         products_of(0, (0, 1, 2, 3))
         multiply(2, (0, 1, 2, 3))
         sum_heads(1)
         negate_mean(1)
-        square_heads(0)
         invert_std(0)
         regroup(nc.scalar.copy, 3, 0)
         regroup(nc.scalar.copy, 3, 1)
         tick(0)
-        regroup_on_gpsimd(3, 3, RIGHT)
+        regroup_on_gpsimd(3, 3, slice(128, 384))
         products_of(1, (3,))
         shift_to_psum()
         products_of(1, (0, 1, 2))
         sum_heads(2)
         negate_mean(2)
         regroup_on_tensor(4, 1, (4, 5))
+        square_heads(1, (0, 1))
         regroup_on_tensor(4, 2, (6, 4))
-        square_heads(1)
+        square_heads(1, (2, 3))
         invert_std(1)
-        regroup(nc.scalar.copy, 4, 0, LEFT)
+        regroup(nc.scalar.copy, 4, 0)
         finish(0)
-        quantise_passes(3, (0, 1, 3, 2))
+        regroup(nc.vector.tensor_copy, 3, 3, slice(384, 512))
+        quantise_passes(3, (0, 1, 2, 3))
         multiply(3, (0, 1, 2))
         tick(1)
         regroup_on_gpsimd(4, 3, LEFT)
@@ -480,12 +547,12 @@ def tile_gqa_flashattn_pa_kernel(
         sum_heads(3)
         negate_mean(3)
         regroup_on_tensor(5, 1, (1, 2))
+        square_heads(2, (0, 1))
         regroup_on_tensor(5, 2, (3, 1))
-        square_heads(2)
+        square_heads(2, (2, 3))
         invert_std(2)
-        regroup(nc.scalar.copy, 5, 0, LEFT)
+        regroup(nc.scalar.copy, 5, 0)
         finish(1)
-        regroup(nc.vector.tensor_copy, 4, 0, RIGHT)
         regroup(nc.vector.tensor_copy, 4, 3, RIGHT)
         quantise_passes(4, (0, 1, 2, 3))
         multiply(4, (0, 1, 2))
@@ -499,7 +566,6 @@ def tile_gqa_flashattn_pa_kernel(
         square_heads(3)
         invert_std(3)
         finish(2)
-        regroup(nc.vector.tensor_copy, 5, 0, RIGHT)
         regroup(nc.vector.tensor_copy, 5, 3, RIGHT)
         quantise_passes(5, (0, 1, 2, 3))
         multiply(5, (0, 1, 2))
@@ -507,10 +573,12 @@ def tile_gqa_flashattn_pa_kernel(
         products_of(4, (0,))
         multiply(5, (3,))
         products_of(4, (1, 2, 3))
+        square_heads(4, (0, 1))
         copy_values(5)
-        square_heads(4)
+        square_heads(4, (2, 3))
         invert_std(4)
-        add_units(nc.gpsimd, 4, HALVES[0])
+        add_units(nc.gpsimd, 4, slice(0, LAST_SHARE))
         finish(3)
-        add_units(nc.vector, 4, HALVES[1])
+        store_values(5)
+        add_units(nc.vector, 4, slice(LAST_SHARE, UNITS))
         finish(4)

@@ -100,13 +100,13 @@ def tile_gqa_flashattn_pa_kernel(
         make_identity(nc, ident_bf[:])
         ones = const.tile([P, P], BF16)
         nc.vector.memset(ones[:], 1.0)
-        for v, vec in ((1, q_beta), (3, k_beta), (0, q_gamma), (2, k_gamma)):
-            nc.scalar.dma_start(
-                out=vector_rows[0:1, v * HEAD : (v + 1) * HEAD], in_=vec.unsqueeze(0)
-            )
         cos_sb = const.tile([P, TOKEN_TILES, HEAD], BF16)
         sin_sb = const.tile([P, TOKEN_TILES, HEAD], BF16)
         nc.sync.dma_start(out=cos_sb[:], in_=cos.rearrange("(p i) j -> p i j", i=TOKEN_TILES))
+        for v, vec in ((1, q_beta), (3, k_beta), (0, q_gamma), (2, k_gamma)):
+            nc.sync.dma_start(
+                out=vector_rows[0:1, v * HEAD : (v + 1) * HEAD], in_=vec.unsqueeze(0)
+            )
         nc.sync.dma_start(out=sin_sb[:], in_=sin.rearrange("(p i) j -> p i j", i=TOKEN_TILES))
 
         raw_tiles = {}

@@ -28,6 +28,7 @@ EPS = 1e-6
 AHEAD = 2
 RAW_TILES = 16
 LAST_SHARE = 6
+SHARE = 320
 RING = 7
 
 FLOPS = 2 * TOKENS * D_MODEL * (Q_BLOCKS + 2) * BLOCK
@@ -79,16 +80,18 @@ def tile_gqa_flashattn_pa_kernel(
         blocks.append((Wk, heads_of(k_rot), "k"))
         blocks.append((Wv, heads_of(v_out), None))
 
-        def store_head(b, h, result):
+        def store_head(b, h, result, tiles=slice(0, TOKEN_TILES)):
             nc.sync.dma_start(
-                out=blocks[b][1][:, h, :],
-                in_=result[:, h * TOKEN_TILES : (h + 1) * TOKEN_TILES, :].rearrange(
-                    "p i j -> p (i j)"
-                ),
+                out=blocks[b][1][:, h, tiles.start * HEAD : tiles.stop * HEAD],
+                in_=result[
+                    :, h * TOKEN_TILES + tiles.start : h * TOKEN_TILES + tiles.stop, :
+                ].rearrange("p i j -> p (i j)"),
             )
 
         vector_rows = const.tile([P, 4 * HEAD], BF16)
-        nc.vector.memset(vector_rows[:], 0.0)
+        VECTORS = ((1, q_beta), (3, k_beta), (0, q_gamma), (2, k_gamma))
+        for v, vec in VECTORS:
+            nc.vector.memset(vector_rows[:, v * HEAD : (v + 1) * HEAD], 0.0)
         eps = const.tile([P, 1], F32)
         nc.vector.memset(eps[:], EPS)
         warm = const.tile([P, 1], F32)
@@ -103,7 +106,7 @@ def tile_gqa_flashattn_pa_kernel(
         cos_sb = const.tile([P, TOKEN_TILES, HEAD], BF16)
         sin_sb = const.tile([P, TOKEN_TILES, HEAD], BF16)
         nc.sync.dma_start(out=cos_sb[:], in_=cos.rearrange("(p i) j -> p i j", i=TOKEN_TILES))
-        for v, vec in ((1, q_beta), (3, k_beta), (0, q_gamma), (2, k_gamma)):
+        for v, vec in VECTORS:
             nc.sync.dma_start(
                 out=vector_rows[0:1, v * HEAD : (v + 1) * HEAD], in_=vec.unsqueeze(0)
             )
@@ -152,14 +155,17 @@ def tile_gqa_flashattn_pa_kernel(
             x_sb = stage.tile([P, TOKEN_TILES * D_MODEL], BF16)
             x_rows = x.rearrange("o (p i) k -> p (o i) k", i=TOKEN_TILES)
             for i in range(TOKEN_TILES):
-                nc.sync.dma_start(
-                    out=x_sb[:, i * D_MODEL : (i + 1) * D_MODEL], in_=x_rows[:, i, :]
-                )
+                for half in range(2):
+                    k0 = half * D_MODEL // 2
+                    nc.sync.dma_start(
+                        out=x_sb[:, i * D_MODEL + k0 : i * D_MODEL + k0 + D_MODEL // 2],
+                        in_=x_rows[:, i, k0 : k0 + D_MODEL // 2],
+                    )
             for b in range(RAW_TILES // PASSES):
                 load_block(b)
 
             spread_ps = bank_tile(0, "spread_ps")
-            for v in (1, 3, 0, 2):
+            for v, vec in VECTORS:
                 part = slice(v * HEAD, (v + 1) * HEAD)
                 nc.tensor.matmul(
                     out=spread_ps[:, part],
@@ -296,10 +302,12 @@ def tile_gqa_flashattn_pa_kernel(
         sums_of = {}
         squares_of = {}
 
-        def sum_heads(b):
-            sums = stats_pool.tile([P, UNITS], F32, name="sums")
-            copies[b] = copies_pool.tile([P, UNITS, HEAD], F32, name="copies")
-            for i in range(TOKEN_TILES):
+        def sum_heads(b, tiles=range(TOKEN_TILES)):
+            if b not in sums_of:
+                sums_of[b] = stats_pool.tile([P, UNITS], F32, name="sums")
+                copies[b] = copies_pool.tile([P, UNITS, HEAD], F32, name="copies")
+            sums = sums_of[b]
+            for i in tiles:
                 for h in range(BLOCK_HEADS):
                     unit = h * TOKEN_TILES + i
                     nc.scalar.activation(
@@ -308,7 +316,6 @@ def tile_gqa_flashattn_pa_kernel(
                         func=ACT.Identity,
                         accum_out=sums[:, unit : unit + 1],
                     )
-            sums_of[b] = sums
 
         def negate_mean(b):
             neg_mean = stats_pool.tile([P, UNITS], F32, name="neg_mean")
@@ -387,19 +394,22 @@ def tile_gqa_flashattn_pa_kernel(
             )
             rstds[b] = rstd
 
-        def copy_values(b):
-            values = result_pool.tile([P, UNITS, HEAD], F32, name="result")
-            by_tile = values[:].rearrange("p (h i) j -> p h i j", i=TOKEN_TILES)
-            for i in range(TOKEN_TILES):
+        def copy_values(b, tiles):
+            if b not in values_of:
+                values_of[b] = result_pool.tile([P, UNITS, HEAD], F32, name="result")
+            by_tile = values_of[b][:].rearrange("p (h i) j -> p h i j", i=TOKEN_TILES)
+            for i in tiles:
                 nc.scalar.copy(
                     out=by_tile[:, :, i, :],
                     in_=banks[(b, i)][:].rearrange("p (h j) -> p h j", h=BLOCK_HEADS),
                 )
-            values_of[b] = values
 
-        def store_values(b):
-            for h in range(BLOCK_HEADS):
-                store_head(b, h, values_of[b])
+        def store_values(b, tiles):
+            by_tile = values_of[b][:].rearrange("p (h i) j -> p h i j", i=TOKEN_TILES)
+            for i in tiles:
+                nc.sync.dma_start(
+                    out=blocks[b][1][:, :, i * HEAD : (i + 1) * HEAD], in_=by_tile[:, :, i, :]
+                )
 
         LEFT, RIGHT = slice(0, BLOCK // 2), slice(BLOCK // 2, BLOCK)
 
@@ -420,7 +430,10 @@ def tile_gqa_flashattn_pa_kernel(
                         op0=ALU.mult,
                         op1=ALU.add,
                     )
-                store_head(b, h, result)
+                    if b == len(blocks) - 2 and h == BLOCK_HEADS - 1 and i % 2 == 1:
+                        store_head(b, h, result, slice(i - 1, i + 1))
+                if b < len(blocks) - 2 or h < BLOCK_HEADS - 1:
+                    store_head(b, h, result)
 
         rstds = {}
 
@@ -490,10 +503,11 @@ def tile_gqa_flashattn_pa_kernel(
 
         regroup(nc.scalar.copy, 0, 1)
         regroup(nc.scalar.copy, 0, 2)
+        quantise_passes(0, (0,))
         regroup(nc.vector.tensor_copy, 0, 3)
-        quantise_passes(0, (0, 3, 1, 2))
+        quantise_passes(0, (3, 1, 2))
         regroup(nc.scalar.copy, 1, 0)
-        regroup(nc.scalar.copy, 1, 1)
+        regroup_on_tensor(1, 1, (5, 6))
         multiply(0, (0, 1, 2, 3))
         regroup(nc.vector.tensor_copy, 1, 2)
         regroup(nc.vector.tensor_copy, 1, 3)
@@ -503,18 +517,19 @@ def tile_gqa_flashattn_pa_kernel(
         multiply(1, (0, 1, 2, 3))
         load_next(1)
         hold_gpsimd(2, 2)
-        regroup_on_gpsimd(2, 2, LEFT)
+        regroup_on_gpsimd(2, 2, slice(0, SHARE))
         bn_heads(0)
         join_moments(0)
-        regroup(nc.vector.tensor_copy, 2, 3)
         bn_mean(0)
-        regroup(nc.vector.tensor_copy, 2, 2, RIGHT)
+        regroup(nc.vector.tensor_copy, 2, 2, slice(SHARE, BLOCK))
         bn_squares(0)
         regroup(nc.scalar.copy, 2, 1)
-        quantise_passes(2, (3, 0, 1, 2))
+        regroup(nc.scalar.copy, 2, 3)
+        quantise_passes(2, (2, 0, 1, 3))
         hold_gpsimd(3, 2)
-        regroup_on_gpsimd(3, 2, slice(0, BLOCK))
-        regroup_on_gpsimd(3, 3, slice(0, 128))
+        regroup_on_gpsimd(3, 2, LEFT)
+        regroup_on_gpsimd(3, 2, RIGHT)
+        regroup_on_gpsimd(3, 3, LEFT)
         products_of(0, (0, 1, 2, 3))
         multiply(2, (0, 1, 2, 3))
         sum_heads(1)
@@ -523,7 +538,7 @@ def tile_gqa_flashattn_pa_kernel(
         regroup(nc.scalar.copy, 3, 0)
         regroup(nc.scalar.copy, 3, 1)
         tick(0)
-        regroup_on_gpsimd(3, 3, slice(128, 384))
+        regroup_on_gpsimd(3, 3, RIGHT)
         products_of(1, (3,))
         shift_to_psum()
         products_of(1, (0, 1, 2))
@@ -536,11 +551,10 @@ def tile_gqa_flashattn_pa_kernel(
         invert_std(1)
         regroup(nc.scalar.copy, 4, 0)
         finish(0)
-        regroup(nc.vector.tensor_copy, 3, 3, slice(384, 512))
         quantise_passes(3, (0, 1, 2, 3))
         multiply(3, (0, 1, 2))
         tick(1)
-        regroup_on_gpsimd(4, 3, LEFT)
+        regroup_on_gpsimd(4, 3, slice(0, SHARE))
         products_of(2, (0,))
         multiply(3, (3,))
         products_of(2, (1, 2, 3))
@@ -553,11 +567,11 @@ def tile_gqa_flashattn_pa_kernel(
         invert_std(2)
         regroup(nc.scalar.copy, 5, 0)
         finish(1)
-        regroup(nc.vector.tensor_copy, 4, 3, RIGHT)
+        regroup(nc.vector.tensor_copy, 4, 3, slice(SHARE, BLOCK))
         quantise_passes(4, (0, 1, 2, 3))
         multiply(4, (0, 1, 2))
         tick(2)
-        regroup_on_gpsimd(5, 3, LEFT)
+        regroup_on_gpsimd(5, 3, slice(0, SHARE))
         products_of(3, (0,))
         multiply(4, (3,))
         products_of(3, (1, 2, 3))
@@ -566,7 +580,7 @@ def tile_gqa_flashattn_pa_kernel(
         square_heads(3)
         invert_std(3)
         finish(2)
-        regroup(nc.vector.tensor_copy, 5, 3, RIGHT)
+        regroup(nc.vector.tensor_copy, 5, 3, slice(SHARE, BLOCK))
         quantise_passes(5, (0, 1, 2, 3))
         multiply(5, (0, 1, 2))
         tick(3)
@@ -574,11 +588,13 @@ def tile_gqa_flashattn_pa_kernel(
         multiply(5, (3,))
         products_of(4, (1, 2, 3))
         square_heads(4, (0, 1))
-        copy_values(5)
+        copy_values(5, (0, 1, 2))
+        store_values(5, (0, 1, 2))
         square_heads(4, (2, 3))
         invert_std(4)
+        copy_values(5, (3,))
         add_units(nc.gpsimd, 4, slice(0, LAST_SHARE))
         finish(3)
-        store_values(5)
+        store_values(5, (3,))
         add_units(nc.vector, 4, slice(LAST_SHARE, UNITS))
         finish(4)

@@ -28,7 +28,7 @@ EPS = 1e-6
 AHEAD = 2
 RAW_TILES = 16
 LAST_SHARE = 6
-SHARE = 320
+SHARE = 384
 RING = 7
 
 FLOPS = 2 * TOKENS * D_MODEL * (Q_BLOCKS + 2) * BLOCK
@@ -155,11 +155,12 @@ def tile_gqa_flashattn_pa_kernel(
             x_sb = stage.tile([P, TOKEN_TILES * D_MODEL], BF16)
             x_rows = x.rearrange("o (p i) k -> p (o i) k", i=TOKEN_TILES)
             for i in range(TOKEN_TILES):
-                for half in range(2):
-                    k0 = half * D_MODEL // 2
+                parts = 2 if i == 0 else 1
+                for part in range(parts):
+                    k0, k1 = part * D_MODEL // parts, (part + 1) * D_MODEL // parts
                     nc.sync.dma_start(
-                        out=x_sb[:, i * D_MODEL + k0 : i * D_MODEL + k0 + D_MODEL // 2],
-                        in_=x_rows[:, i, k0 : k0 + D_MODEL // 2],
+                        out=x_sb[:, i * D_MODEL + k0 : i * D_MODEL + k1],
+                        in_=x_rows[:, i, k0:k1],
                     )
             for b in range(RAW_TILES // PASSES):
                 load_block(b)
@@ -447,8 +448,7 @@ def tile_gqa_flashattn_pa_kernel(
         FULL = slice(0, BLOCK)
 
         def tick(b):
-            values = rotated[b][0][:, UNITS // 2 - 1 :: UNITS // 2, 1, HEAD - 1 : HEAD]
-            nc.vector.tensor_scalar_mul(out=values, in0=values, scalar1=1.0)
+            nc.vector.memset(rotated[b][1][:, UNITS // 2 - 1 :: UNITS // 2, 0:1], 0.0)
             for units in HALVES:
                 add_units(nc.gpsimd, b, units)
 
@@ -505,7 +505,8 @@ def tile_gqa_flashattn_pa_kernel(
         regroup(nc.scalar.copy, 0, 2)
         quantise_passes(0, (0,))
         regroup(nc.vector.tensor_copy, 0, 3)
-        quantise_passes(0, (3, 1, 2))
+        quantise_passes(0, (1,))
+        quantise_passes(0, (3, 2))
         regroup(nc.scalar.copy, 1, 0)
         regroup_on_tensor(1, 1, (5, 6))
         multiply(0, (0, 1, 2, 3))
@@ -517,15 +518,17 @@ def tile_gqa_flashattn_pa_kernel(
         multiply(1, (0, 1, 2, 3))
         load_next(1)
         hold_gpsimd(2, 2)
-        regroup_on_gpsimd(2, 2, slice(0, SHARE))
-        bn_heads(0)
-        join_moments(0)
-        bn_mean(0)
-        regroup(nc.vector.tensor_copy, 2, 2, slice(SHARE, BLOCK))
-        bn_squares(0)
+        regroup_on_gpsimd(2, 2, slice(0, BLOCK))
         regroup(nc.scalar.copy, 2, 1)
         regroup(nc.scalar.copy, 2, 3)
-        quantise_passes(2, (2, 0, 1, 3))
+        bn_heads(0)
+        quantise_passes(2, (0,))
+        join_moments(0)
+        quantise_passes(2, (1,))
+        bn_mean(0)
+        quantise_passes(2, (2,))
+        bn_squares(0)
+        quantise_passes(2, (3,))
         hold_gpsimd(3, 2)
         regroup_on_gpsimd(3, 2, LEFT)
         regroup_on_gpsimd(3, 2, RIGHT)
@@ -539,12 +542,13 @@ def tile_gqa_flashattn_pa_kernel(
         regroup(nc.scalar.copy, 3, 1)
         tick(0)
         regroup_on_gpsimd(3, 3, RIGHT)
+        regroup_on_gpsimd(4, 3, slice(0, 128))
         products_of(1, (3,))
         shift_to_psum()
         products_of(1, (0, 1, 2))
         sum_heads(2)
-        negate_mean(2)
         regroup_on_tensor(4, 1, (4, 5))
+        negate_mean(2)
         square_heads(1, (0, 1))
         regroup_on_tensor(4, 2, (6, 4))
         square_heads(1, (2, 3))
@@ -554,7 +558,7 @@ def tile_gqa_flashattn_pa_kernel(
         quantise_passes(3, (0, 1, 2, 3))
         multiply(3, (0, 1, 2))
         tick(1)
-        regroup_on_gpsimd(4, 3, slice(0, SHARE))
+        regroup_on_gpsimd(4, 3, slice(128, 512))
         products_of(2, (0,))
         multiply(3, (3,))
         products_of(2, (1, 2, 3))
@@ -567,7 +571,6 @@ def tile_gqa_flashattn_pa_kernel(
         invert_std(2)
         regroup(nc.scalar.copy, 5, 0)
         finish(1)
-        regroup(nc.vector.tensor_copy, 4, 3, slice(SHARE, BLOCK))
         quantise_passes(4, (0, 1, 2, 3))
         multiply(4, (0, 1, 2))
         tick(2)

from contextlib import ExitStack

import concourse.mybir as mybir
from concourse.masks import make_identity

F32 = mybir.dt.float32
BF16 = mybir.dt.bfloat16
U32 = mybir.dt.uint32
U8 = mybir.dt.uint8
FP8X4 = mybir.dt.float8_e4m3fn_x4
ALU = mybir.AluOpType
ACT = mybir.ActivationFunctionType

P = 128
PACK = 4
K_PASS = P * PACK
TOKENS = 512
TOKEN_TILES = TOKENS // P
D_MODEL = 2048
PASSES = D_MODEL // K_PASS
HEAD = 128
HALF = HEAD // 2
BLOCK_HEADS = 4
BLOCK = BLOCK_HEADS * HEAD
UNITS = BLOCK_HEADS * TOKEN_TILES
Q_BLOCKS = 4
EPS = 1e-6
AHEAD = 2
RAW_TILES = 16
LAST_SHARE = 6
SHARE = 384
RING = 7

FLOPS = 2 * TOKENS * D_MODEL * (Q_BLOCKS + 2) * BLOCK


def add_partner_halves(engine, out, products):
    halves = "p n (s e) -> p n s e"
    engine.tensor_tensor(
        out=out[:, :, :].rearrange(halves, s=2),
        in0=products[:, :, 0, :].rearrange(halves, s=2),
        in1=products[:, :, 1, :].rearrange(halves, s=2)[:, :, ::-1, :],
        op=ALU.add,
    )


def tile_gqa_flashattn_pa_kernel(
    tc, x, cos, sin, Wq, Wk, Wv, q_gamma, q_beta, k_gamma, k_beta, q_rot, k_rot, v_out
):
    nc = tc.nc
    with ExitStack() as ctx:
        ctx.enter_context(tc.manual_schedule())
        const = ctx.enter_context(tc.tile_pool(name="const", bufs=1))
        raw_pool = ctx.enter_context(tc.tile_pool(name="raw", bufs=RAW_TILES))
        grouped_pool = ctx.enter_context(tc.tile_pool(name="grouped", bufs=1))
        codes_pool = ctx.enter_context(tc.tile_pool(name="codes", bufs=3))
        stats_pool = ctx.enter_context(tc.tile_pool(name="stats", bufs=4))
        psum = ctx.enter_context(tc.psum_pool(name="psum", bufs=1))

        def bank_tile(n, name, width=P * PACK, dtype=F32):
            return psum.tile([P, width], dtype, tag="bank%d" % n, name=name)

        def bank_of(b, i):
            if b < 2:
                return TOKEN_TILES * b + i
            return (TOKEN_TILES * (b - 2) + i) % RING

        def heads_of(out):
            return out.rearrange("o h (p i) j -> p (o h) (i j)", i=TOKEN_TILES)

        blocks = []
        for c in range(Q_BLOCKS):
            blocks.append(
                (
                    Wq[:, c * BLOCK : (c + 1) * BLOCK],
                    heads_of(q_rot)[:, c * BLOCK_HEADS : (c + 1) * BLOCK_HEADS, :],
                    "q",
                )
            )
        blocks.append((Wk, heads_of(k_rot), "k"))
        blocks.append((Wv, heads_of(v_out), None))

        def store_head(b, h, result, tiles=slice(0, TOKEN_TILES)):
            nc.sync.dma_start(
                out=blocks[b][1][:, h, tiles.start * HEAD : tiles.stop * HEAD],
                in_=result[
                    :, h * TOKEN_TILES + tiles.start : h * TOKEN_TILES + tiles.stop, :
                ].rearrange("p i j -> p (i j)"),
            )

        vector_rows = const.tile([P, 4 * HEAD], BF16)
        VECTORS = ((1, q_beta), (3, k_beta), (0, q_gamma), (2, k_gamma))
        for v, vec in VECTORS:
            nc.vector.memset(vector_rows[:, v * HEAD : (v + 1) * HEAD], 0.0)
        eps = const.tile([P, 1], F32)
        nc.vector.memset(eps[:], EPS)
        warm = const.tile([P, 1], F32)
        nc.scalar.activation(out=warm[:], in_=eps[:], func=ACT.Abs_reciprocal_sqrt)

        ident = const.tile([P, P], F32)
        make_identity(nc, ident[:])
        ident_bf = const.tile([P, P], BF16)
        make_identity(nc, ident_bf[:])
        ones = const.tile([P, P], BF16)
        nc.vector.memset(ones[:], 1.0)
        cos_sb = const.tile([P, TOKEN_TILES, HEAD], BF16)
        sin_sb = const.tile([P, TOKEN_TILES, HEAD], BF16)
        nc.sync.dma_start(out=cos_sb[:], in_=cos.rearrange("(p i) j -> p i j", i=TOKEN_TILES))
        for v, vec in VECTORS:
            nc.sync.dma_start(
                out=vector_rows[0:1, v * HEAD : (v + 1) * HEAD], in_=vec.unsqueeze(0)
            )
        nc.sync.dma_start(out=sin_sb[:], in_=sin.rearrange("(p i) j -> p i j", i=TOKEN_TILES))

        raw_tiles = {}

        def load_block(b):
            rows = blocks[b][0].rearrange("(g p t) n -> g p t n", g=PASSES, t=PACK)
            for g in range(PASSES):
                raw = raw_pool.tile([P, PACK, BLOCK], BF16, name="raw")
                nc.sync.dma_start(out=raw[:], in_=rows[g])
                raw_tiles[(b, g)] = raw

        factors = {}
        shifts = {}
        for kind in ("k", "q"):
            factors[kind] = const.tile([P, TOKEN_TILES, 2, HEAD], F32, name="factors_" + kind)
            shifts[kind] = const.tile([P, TOKEN_TILES, HEAD], F32, name="shift_" + kind)
        LEFT, RIGHT = slice(0, BLOCK // 2), slice(BLOCK // 2, BLOCK)
        x_codes = const.tile([P, TOKEN_TILES, PASSES * P], U32, align_bytes=64)
        x_scales = const.tile([P, TOKEN_TILES, PASSES * P], U8, align_bytes=64)

        grouped_tiles = {}
        early = set()

        def grouped_tile(b, g):
            if (b, g) not in grouped_tiles:
                grouped = grouped_pool.tile(
                    [P, BLOCK, PACK],
                    BF16,
                    align_bytes=64,
                    tag="grouped%d" % (PASSES * (b % 2) + g),
                    name="grouped",
                )
                grouped_tiles[(b, g)] = grouped
            return grouped_tiles[(b, g)]

        def regroup(engine_copy, b, g, columns=slice(0, BLOCK)):
            engine_copy(
                out=grouped_tile(b, g)[:, columns, :].rearrange("p (c r) t -> p c t r", r=4),
                in_=raw_tiles[(b, g)][:, :, columns].rearrange("p t (c r) -> p c t r", r=4),
            )

        with tc.tile_pool(name="stage", bufs=1) as stage:
            x_sb = stage.tile([P, TOKEN_TILES * D_MODEL], BF16)
            x_rows = x.rearrange("o (p i) k -> p (o i) k", i=TOKEN_TILES)
            for i in range(TOKEN_TILES):
                parts = 2 if i == 0 else 1
                for part in range(parts):
                    k0, k1 = part * D_MODEL // parts, (part + 1) * D_MODEL // parts
                    nc.sync.dma_start(
                        out=x_sb[:, i * D_MODEL + k0 : i * D_MODEL + k1],
                        in_=x_rows[:, i, k0:k1],
                    )
            for b in range(RAW_TILES // PASSES):
                load_block(b)

            spread_ps = bank_tile(0, "spread_ps")
            for v, vec in VECTORS:
                part = slice(v * HEAD, (v + 1) * HEAD)
                nc.tensor.matmul(
                    out=spread_ps[:, part],
                    lhsT=ones[:],
                    rhs=vector_rows[:, part],
                    start=True,
                    stop=True,
                )
            spread = spread_ps[:].rearrange("p (v j) -> p v j", v=4)

            def rotation_products(out, v):
                def over_tiles(ap):
                    return ap.unsqueeze(1).to_broadcast([P, TOKEN_TILES, ap.shape[1]])

                nc.vector.tensor_tensor(
                    out=out[:, :, 0, :], in0=cos_sb[:], in1=over_tiles(spread[:, v, :]), op=ALU.mult
                )
                for lo, partner, sign in ((0, HALF, 1.0), (HALF, 0, -1.0)):
                    nc.vector.scalar_tensor_tensor(
                        out=out[:, :, 1, lo : lo + HALF],
                        in0=sin_sb[:, :, partner : partner + HALF],
                        scalar=sign,
                        in1=over_tiles(spread[:, v, lo : lo + HALF]),
                        op0=ALU.mult,
                        op1=ALU.mult,
                    )

            for kind, v in (("q", 0), ("k", 2)):
                beta_products = stage.tile([P, TOKEN_TILES, 2, HEAD], F32, name="beta_" + kind)
                rotation_products(beta_products, v + 1)
                add_partner_halves(nc.gpsimd, shifts[kind], beta_products)
            for kind, v in (("q", 0), ("k", 2)):
                rotation_products(factors[kind], v)

            x_words = x_sb[:].bitcast(F32).rearrange(
                "p (i g m u) -> p i g u m", i=TOKEN_TILES, g=PASSES, u=2
            )
            x_grouped = []
            for i in range(TOKEN_TILES):
                grouped = stage.tile(
                    [P, PASSES * P * PACK], BF16, align_bytes=64, name="x_grouped%d" % i
                )
                x_grouped.append(grouped)
                grouped_words = grouped[:].bitcast(F32).rearrange(
                    "p (g s u) -> p g s u", g=PASSES, u=2
                )
                for pair in range(PASSES // 2):
                    xt = bank_tile(RING - 4 + (2 * i + pair) % 4, "xt")
                    for g2 in range(2):
                        for u in range(2):
                            nc.tensor.transpose(
                                xt[:, (2 * g2 + u) * P : (2 * g2 + u + 1) * P],
                                x_words[:, i, 2 * pair + g2, u, :],
                                ident[:],
                            )
                    nc.scalar.copy(
                        out=grouped_words[:, 2 * pair : 2 * pair + 2, :, :],
                        in_=xt[:].rearrange("p (g u s) -> p g s u", g=2, u=2),
                    )
            for i in range(TOKEN_TILES):
                nc.vector.quantize_mx(
                    out=x_codes[:, i, :].bitcast(FP8X4),
                    scales=x_scales[:, i, :],
                    in_=x_grouped[i][:],
                )
                if i == 1:
                    regroup(nc.vector.tensor_copy, 0, 0)
                    early.add((0, 0))

        late = ctx.enter_context(tc.tile_pool(name="late", bufs=1))
        products_pool = ctx.enter_context(tc.tile_pool(name="products", bufs=2))
        result_pool = ctx.enter_context(tc.tile_pool(name="result", bufs=3))
        unread = late.tile([P, UNITS, HEAD], BF16)
        copies_pool = ctx.enter_context(tc.tile_pool(name="copies", bufs=2))
        copies = {}
        banks = {}
        neg_means = {}
        stats = {}
        rotated = {}

        def head_sums(b, i, h):
            return banks[(b, i)][:, h * HEAD : (h + 1) * HEAD]

        codes = {}

        def regroup_on_gpsimd(b, g, columns):
            nc.gpsimd.tensor_scalar(
                out=grouped_tile(b, g)[:, columns, :],
                in0=raw_tiles[(b, g)][:, :, columns].rearrange("p t n -> p n t"),
                scalar1=1.0,
                scalar2=0.0,
                op0=ALU.mult,
                op1=ALU.add,
            )

        def regroup_on_tensor(b, g, bank_numbers):
            flat = grouped_tile(b, g)[:].rearrange("p n t -> p (n t)")
            raw = raw_tiles[(b, g)]
            for half in range(2):
                mixed = bank_tile(bank_numbers[half], "mixed", 2 * BLOCK, BF16)
                for q in range(2):
                    c0 = (2 * half + q) * P
                    nc.tensor.matmul(
                        out=mixed[:, q * BLOCK : (q + 1) * BLOCK].rearrange(
                            "p (c t) -> p t c", t=PACK
                        ),
                        lhsT=ident_bf[:],
                        rhs=raw[:, :, c0 : c0 + P],
                        start=True,
                        stop=True,
                    )
                nc.scalar.copy(
                    out=flat[:, half * 2 * BLOCK : (half + 1) * 2 * BLOCK].bitcast(F32),
                    in_=mixed[:].bitcast(F32),
                )

        def multiply(b, tiles):
            w_codes, w_scales = codes[b]
            for i in tiles:
                bank = bank_tile(bank_of(b, i), "bank")
                banks[(b, i)] = bank
                for g in range(PASSES):
                    nc.tensor.matmul_mx(
                        out=bank[:],
                        lhsT=x_codes[:, i, g * P : (g + 1) * P].bitcast(FP8X4),
                        lhsT_scale=x_scales[:, i, g * P : (g + 1) * P],
                        rhs=w_codes[:, g, :].bitcast(FP8X4),
                        rhs_scale=w_scales[:, g, :],
                        start=(g == 0),
                        stop=(g == PASSES - 1),
                    )

        values_of = {}
        sums_of = {}
        squares_of = {}

        def sum_heads(b, tiles=range(TOKEN_TILES)):
            if b not in sums_of:
                sums_of[b] = stats_pool.tile([P, UNITS], F32, name="sums")
                copies[b] = copies_pool.tile([P, UNITS, HEAD], F32, name="copies")
            sums = sums_of[b]
            for i in tiles:
                for h in range(BLOCK_HEADS):
                    unit = h * TOKEN_TILES + i
                    nc.scalar.activation(
                        out=copies[b][:, unit, :],
                        in_=head_sums(b, i, h),
                        func=ACT.Identity,
                        accum_out=sums[:, unit : unit + 1],
                    )

        def negate_mean(b):
            neg_mean = stats_pool.tile([P, UNITS], F32, name="neg_mean")
            nc.scalar.mul(out=neg_mean[:], in_=sums_of[b][:], mul=-1.0 / HEAD)
            neg_means[b] = neg_mean

        def square_heads(b, tiles=range(TOKEN_TILES)):
            neg_mean = neg_means[b]
            if b not in squares_of:
                squares_of[b] = stats_pool.tile([P, UNITS], F32, name="squares")
            squares = squares_of[b]
            for i in tiles:
                for h in range(BLOCK_HEADS):
                    unit = h * TOKEN_TILES + i
                    nc.scalar.activation(
                        out=unread[:, unit, :],
                        in_=copies[b][:, unit, :],
                        func=ACT.Square,
                        bias=neg_mean[:, unit : unit + 1],
                        accum_out=squares[:, unit : unit + 1],
                    )

        moments_of = {}
        spreads_of = {}

        def bn_heads(b, tiles=range(TOKEN_TILES)):
            if b not in moments_of:
                moments_of[b] = stats_pool.tile([P, UNITS, 6], F32, name="moments")
            for i in tiles:
                for h in range(BLOCK_HEADS):
                    nc.vector.bn_stats(
                        out=moments_of[b][:, h * TOKEN_TILES + i, :], in_=head_sums(b, i, h)
                    )

        def join_moments(b):
            moments = moments_of[b]
            total = stats_pool.tile([P, UNITS], F32, name="total")
            nc.vector.tensor_tensor(
                out=total[:], in0=moments[:, :, 1], in1=moments[:, :, 4], op=ALU.add
            )
            gap = stats_pool.tile([P, UNITS], F32, name="gap")
            nc.vector.tensor_tensor(
                out=gap[:], in0=moments[:, :, 1], in1=moments[:, :, 4], op=ALU.subtract
            )
            within = stats_pool.tile([P, UNITS], F32, name="within")
            nc.vector.tensor_tensor(
                out=within[:], in0=moments[:, :, 2], in1=moments[:, :, 5], op=ALU.add
            )
            spreads_of[b] = (total, gap, within)

        def bn_mean(b):
            total, gap, within = spreads_of[b]
            neg_mean = stats_pool.tile([P, UNITS], F32, name="neg_mean")
            nc.vector.tensor_scalar_mul(out=neg_mean[:], in0=total[:], scalar1=-0.5)
            neg_means[b] = neg_mean
            between = stats_pool.tile([P, UNITS], F32, name="between")
            nc.vector.scalar_tensor_tensor(
                out=between[:], in0=gap[:], scalar=HEAD / 4, in1=gap[:], op0=ALU.mult, op1=ALU.mult
            )
            spreads_of[b] = (between, within)

        def bn_squares(b):
            between, within = spreads_of[b]
            squares = stats_pool.tile([P, UNITS], F32, name="squares")
            nc.vector.tensor_tensor(out=squares[:], in0=within[:], in1=between[:], op=ALU.add)
            squares_of[b] = squares

        def invert_std(b):
            rstd = stats_pool.tile([P, UNITS], F32, name="rstd")
            nc.scalar.activation(
                out=rstd[:],
                in_=squares_of[b][:],
                func=ACT.Abs_reciprocal_sqrt,
                bias=eps[:],
                scale=1.0 / HEAD,
            )
            rstds[b] = rstd

        def copy_values(b, tiles):
            if b not in values_of:
                values_of[b] = result_pool.tile([P, UNITS, HEAD], F32, name="result")
            by_tile = values_of[b][:].rearrange("p (h i) j -> p h i j", i=TOKEN_TILES)
            for i in tiles:
                nc.scalar.copy(
                    out=by_tile[:, :, i, :],
                    in_=banks[(b, i)][:].rearrange("p (h j) -> p h j", h=BLOCK_HEADS),
                )

        def store_values(b, tiles):
            by_tile = values_of[b][:].rearrange("p (h i) j -> p h i j", i=TOKEN_TILES)
            for i in tiles:
                nc.sync.dma_start(
                    out=blocks[b][1][:, :, i * HEAD : (i + 1) * HEAD], in_=by_tile[:, :, i, :]
                )

        LEFT, RIGHT = slice(0, BLOCK // 2), slice(BLOCK // 2, BLOCK)

        def load_next(b):
            if b + RAW_TILES // PASSES < len(blocks):
                load_block(b + RAW_TILES // PASSES)

        def finish(b):
            result = rotated[b][1]
            for h in range(BLOCK_HEADS):
                for i in range(TOKEN_TILES):
                    unit = h * TOKEN_TILES + i
                    nc.vector.scalar_tensor_tensor(
                        out=result[:, unit, :],
                        in0=result[:, unit, :],
                        scalar=rstds[b][:, unit : unit + 1],
                        in1=shifts[blocks[b][2]][:, i, :],
                        op0=ALU.mult,
                        op1=ALU.add,
                    )
                    if b == len(blocks) - 2 and h == BLOCK_HEADS - 1 and i % 2 == 1:
                        store_head(b, h, result, slice(i - 1, i + 1))
                if b < len(blocks) - 2 or h < BLOCK_HEADS - 1:
                    store_head(b, h, result)

        rstds = {}

        HALVES = (slice(0, UNITS // 2), slice(UNITS // 2, UNITS))

        def add_units(engine, b, units):
            products, result = rotated[b]
            add_partner_halves(engine, result[:, units, :], products[:, units, :, :])

        last = len(blocks) - 1
        FULL = slice(0, BLOCK)

        def tick(b):
            nc.vector.memset(rotated[b][1][:, UNITS // 2 - 1 :: UNITS // 2, 0:1], 0.0)
            for units in HALVES:
                add_units(nc.gpsimd, b, units)

        def shift_to_psum():
            shift_ps = bank_tile(RING, "shift_ps")
            nc.tensor.matmul(
                out=shift_ps[:],
                lhsT=ident[:],
                rhs=shifts["q"][:].rearrange("p i j -> p (i j)"),
                start=True,
                stop=True,
            )
            shifts["q"] = shift_ps[:].rearrange("p (i j) -> p i j", i=TOKEN_TILES)

        def products_of(b, tiles):
            if b not in rotated:
                rotated[b] = (
                    products_pool.tile([P, UNITS, 2, HEAD], F32, name="products"),
                    result_pool.tile([P, UNITS, HEAD], F32, name="result"),
                )
            products, result = rotated[b]
            neg_mean = neg_means[b]
            for i in tiles:
                for h in range(BLOCK_HEADS):
                    unit = h * TOKEN_TILES + i
                    nc.vector.scalar_tensor_tensor(
                        out=products[:, unit, :, :],
                        in0=head_sums(b, i, h).unsqueeze(1).to_broadcast([P, 2, HEAD]),
                        scalar=neg_mean[:, unit : unit + 1],
                        in1=factors[blocks[b][2]][:, i, :, :],
                        op0=ALU.add,
                        op1=ALU.mult,
                    )

        def quantise_passes(b, gs):
            if b not in codes:
                w_codes = codes_pool.tile([P, PASSES, BLOCK], U32, align_bytes=64, name="w_codes")
                w_scales = codes_pool.tile([P, PASSES, BLOCK], U8, align_bytes=64, name="w_scales")
                codes[b] = (w_codes, w_scales)
            w_codes, w_scales = codes[b]
            for g in gs:
                nc.vector.quantize_mx(
                    out=w_codes[:, g, :].bitcast(FP8X4),
                    scales=w_scales[:, g, :],
                    in_=grouped_tiles[(b, g)][:].rearrange("p n t -> p (n t)"),
                )

        def hold_gpsimd(b, g):
            nc.vector.tensor_copy(
                out=grouped_tile(b, g)[:, 0:1, 0:1], in_=raw_tiles[(b, g)][:, 0:1, 0:1]
            )

        regroup(nc.scalar.copy, 0, 1)
        regroup(nc.scalar.copy, 0, 2)
        quantise_passes(0, (0,))
        regroup(nc.vector.tensor_copy, 0, 3)
        quantise_passes(0, (1,))
        quantise_passes(0, (3, 2))
        regroup(nc.scalar.copy, 1, 0)
        regroup_on_tensor(1, 1, (5, 6))
        multiply(0, (0, 1, 2, 3))
        regroup(nc.vector.tensor_copy, 1, 2)
        regroup(nc.vector.tensor_copy, 1, 3)
        load_next(0)
        quantise_passes(1, (2, 3, 0, 1))
        regroup(nc.scalar.copy, 2, 0)
        multiply(1, (0, 1, 2, 3))
        load_next(1)
        hold_gpsimd(2, 2)
        regroup_on_gpsimd(2, 2, slice(0, BLOCK))
        regroup(nc.scalar.copy, 2, 1)
        regroup(nc.scalar.copy, 2, 3)
        bn_heads(0)
        quantise_passes(2, (0,))
        join_moments(0)
        quantise_passes(2, (1,))
        bn_mean(0)
        quantise_passes(2, (2,))
        bn_squares(0)
        quantise_passes(2, (3,))
        hold_gpsimd(3, 2)
        regroup_on_gpsimd(3, 2, LEFT)
        regroup_on_gpsimd(3, 2, RIGHT)
        regroup_on_gpsimd(3, 3, LEFT)
        products_of(0, (0, 1, 2, 3))
        multiply(2, (0, 1, 2, 3))
        sum_heads(1)
        negate_mean(1)
        invert_std(0)
        regroup(nc.scalar.copy, 3, 0)
        regroup(nc.scalar.copy, 3, 1)
        tick(0)
        regroup_on_gpsimd(3, 3, RIGHT)
        regroup_on_gpsimd(4, 3, slice(0, 128))
        products_of(1, (3,))
        shift_to_psum()
        products_of(1, (0, 1, 2))
        sum_heads(2)
        regroup_on_tensor(4, 1, (4, 5))
        negate_mean(2)
        square_heads(1, (0, 1))
        regroup_on_tensor(4, 2, (6, 4))
        square_heads(1, (2, 3))
        invert_std(1)
        regroup(nc.scalar.copy, 4, 0)
        finish(0)
        quantise_passes(3, (0, 1, 2, 3))
        multiply(3, (0, 1, 2))
        tick(1)
        regroup_on_gpsimd(4, 3, slice(128, 512))
        products_of(2, (0,))
        multiply(3, (3,))
        products_of(2, (1, 2, 3))
        sum_heads(3)
        negate_mean(3)
        regroup_on_tensor(5, 1, (1, 2))
        square_heads(2, (0, 1))
        regroup_on_tensor(5, 2, (3, 1))
        square_heads(2, (2, 3))
        invert_std(2)
        regroup(nc.scalar.copy, 5, 0)
        finish(1)
        quantise_passes(4, (0, 1, 2, 3))
        multiply(4, (0, 1, 2))
        tick(2)
        regroup_on_gpsimd(5, 3, slice(0, SHARE))
        products_of(3, (0,))
        multiply(4, (3,))
        products_of(3, (1, 2, 3))
        sum_heads(4)
        negate_mean(4)
        square_heads(3)
        invert_std(3)
        finish(2)
        regroup(nc.vector.tensor_copy, 5, 3, slice(SHARE, BLOCK))
        quantise_passes(5, (0, 1, 2, 3))
        multiply(5, (0, 1, 2))
        tick(3)
        products_of(4, (0,))
        multiply(5, (3,))
        products_of(4, (1, 2, 3))
        square_heads(4, (0, 1))
        copy_values(5, (0, 1, 2))
        store_values(5, (0, 1, 2))
        square_heads(4, (2, 3))
        invert_std(4)
        copy_values(5, (3,))
        add_units(nc.gpsimd, 4, slice(0, LAST_SHARE))
        finish(3)
        store_values(5, (3,))
        add_units(nc.vector, 4, slice(LAST_SHARE, UNITS))
        finish(4)
